import numpy as np
import ml_dtypes


def mxq(x, axis, fmt="e4m3"):
    dtype, down = {"e4m3": (ml_dtypes.float8_e4m3fn, 7), "e5m2": (ml_dtypes.float8_e5m2, 14)}[fmt]
    v = np.moveaxis(np.asarray(x, np.float32).astype(ml_dtypes.bfloat16).astype(np.float64), axis, -1)
    blocks = v.reshape(v.shape[:-1] + (-1, 32))
    amax = np.abs(blocks).max(-1, keepdims=True)
    byte = np.maximum(np.where(amax > 0, np.frexp(amax)[1] - 1 + 127, 0) - down, 1)
    scale = np.exp2(byte - 127.0)
    codes = (blocks / scale).astype(np.float32).astype(dtype).astype(np.float64)
    return np.moveaxis((codes * scale).reshape(v.shape), -1, axis)


WIDE = False


def mx_kscale(k):
    if not WIDE:
        return np.ones(k)
    levels = np.array([10, -10, 5, -5, 0])
    a = np.random.permutation(np.resize(levels, k // 512 * 4)).reshape(k // 512, 4)
    idx = np.arange(k)
    return np.exp2(a[idx // 512, idx % 128 // 32])


BF16 = ml_dtypes.bfloat16


def bf(x):
    return np.asarray(x, np.float32).astype(BF16)


def f64(x):
    return np.asarray(x).astype(np.float64)


B, DIN, F, H, K, G = 1024, 512, 512, 512, 7, 3


def sigmoid(v):
    return 1.0 / (1.0 + np.exp(-v))


def setup_inputs():
    s = mx_kscale(DIN)
    return {"hx": bf(np.random.standard_normal((B, DIN)) * s),
            "cx2": bf(np.random.standard_normal((B, H))),
            "w1": bf(np.random.standard_normal((G, F, DIN)) / np.sqrt(DIN) / s),
            "b1": bf(np.random.standard_normal((G, F)) * 0.5),
            "w2": bf(np.random.standard_normal((G, H, F)) * 1.5 / np.sqrt(F)),
            "b2": bf(np.random.standard_normal((G, H)) * 0.5)}


def reference(hx, cx2, w1, b1, w2, b2):
    h1 = (mxq(f64(hx), 1, "e4m3") @ mxq(f64(w1), 2, "e4m3").transpose(0, 2, 1)) + f64(b1)[:, None, :]
    a1 = np.tanh(h1)
    h2 = (mxq(a1, 2, "e4m3") @ mxq(f64(w2), 2, "e4m3").transpose(0, 2, 1)) + f64(b2)[:, None, :]
    i2, f2, zg = sigmoid(np.tanh(h2))
    z = np.tanh(zg)
    return f2 * f64(cx2) + i2 * z

@@ -1,0 +1,248 @@
+from contextlib import ExitStack
+
+import concourse.mybir as mybir
+from concourse.masks import make_identity
+
+FLOPS = 2 * 1024 * 512 * 512 * 6
+
+F32 = mybir.dt.float32
+BF16 = mybir.dt.bfloat16
+U32 = mybir.dt.uint32
+U8 = mybir.dt.uint8
+FP8X4 = mybir.dt.float8_e4m3fn_x4
+ACT = mybir.ActivationFunctionType
+ALU = mybir.AluOpType
+
+P = 128
+GATE_ORDER = (1, 2, 0)
+
+
+def tile_lstmcellunknowndata_pa_kernel(tc, hx, cx2, w1, b1, w2, b2, out):
+    nc = tc.nc
+    with ExitStack() as ctx:
+        keep = ctx.enter_context(tc.tile_pool(name="keep", bufs=1))
+        stage = ctx.enter_context(tc.tile_pool(name="stage", bufs=3))
+        outp = ctx.enter_context(tc.tile_pool(name="outp", bufs=4))
+        psum_mm = ctx.enter_context(tc.psum_pool(name="psmm", bufs=4))
+        psum_tp = ctx.enter_context(tc.psum_pool(name="pstp", bufs=4))
+
+        b1_raw = keep.tile([P, 256], BF16, name="b1_raw")
+        b2_raw = keep.tile([P, P], BF16, name="b2_raw")
+        nc.vector.memset(b1_raw[:], 0.0)
+        nc.vector.memset(b2_raw[:], 0.0)
+        nc.scalar.dma_start(out=b1_raw[0:6, :], in_=b1.rearrange("g (u x) -> (g u) x", u=2))
+        nc.scalar.dma_start(out=b2_raw[0:12, :], in_=b2.rearrange("g (t x) -> (g t) x", t=4))
+        hx_sb = keep.tile([P, 4096], BF16, name="hx_sb")
+        cx_sb = keep.tile([P, 4096], BF16, name="cx_sb")
+        w1_sb = {}
+        w2_sb = {}
+        for g in range(3):
+            w1_sb[g] = keep.tile([P, 2048], BF16, name="w1_sb%d" % g)
+            w2_sb[g] = keep.tile([P, 2048], BF16, name="w2_sb%d" % g)
+        hx_rows = hx.rearrange("(p j) k -> p (j k)", j=8)
+
+        def load_w1(g):
+            nc.sync.dma_start(
+                out=w1_sb[g][:].rearrange("p (u x) -> p u x", u=2),
+                in_=w1[g].rearrange("(u p e) k -> p u (e k)", u=2, e=2),
+            )
+
+        def load_w2(g):
+            nc.sync.dma_start(
+                out=w2_sb[g][:].rearrange("p (t f) -> p t f", t=4),
+                in_=w2[g].rearrange("(t p) f -> p t f", p=P),
+            )
+
+        nc.sync.dma_start(out=hx_sb[:, 0:2048], in_=hx_rows[:, 0:2048])
+        load_w1(GATE_ORDER[0])
+        load_w1(GATE_ORDER[1])
+        load_w1(GATE_ORDER[2])
+        load_w2(GATE_ORDER[0])
+        load_w2(GATE_ORDER[1])
+        load_w2(GATE_ORDER[2])
+        nc.sync.dma_start(out=hx_sb[:, 2048:4096], in_=hx_rows[:, 2048:4096])
+        nc.sync.dma_start(out=cx_sb[:], in_=cx2.rearrange("(p j) h -> p (j h)", j=8))
+
+        warm_in = keep.tile([P, 1], F32, name="warm_in")
+        warm_out = keep.tile([P, 1], F32, name="warm_out")
+        nc.vector.memset(warm_in[:], 0.0)
+        nc.scalar.activation(out=warm_out[:], in_=warm_in[:], func=ACT.Tanh)
+
+        ident = keep.tile([P, P], F32, name="ident")
+        make_identity(nc, ident[:])
+
+        b2_f32 = keep.tile([P, P], F32, name="b2_f32")
+        nc.vector.tensor_copy(out=b2_f32[:], in_=b2_raw[:])
+        b_ps = psum_tp.tile([P, 2, P], F32, name="b_ps", tag="tp")
+        nc.tensor.transpose(b_ps[:, 0, :], b1_raw[:].bitcast(F32), ident[:])
+        nc.tensor.transpose(b_ps[:, 1, :], b2_f32[:], ident[:])
+        b1_words = keep.tile([P, 8], F32, name="b1_words")
+        nc.vector.tensor_copy(out=b1_words[:, 0:6], in_=b_ps[:, 0, 0:6])
+        bias1 = keep.tile([P, 12], F32, name="bias1")
+        nc.vector.tensor_copy(out=bias1[:], in_=b1_words[:, 0:6].bitcast(BF16))
+        bias2 = keep.tile([P, 12], F32, name="bias2")
+        nc.vector.tensor_copy(out=bias2[:], in_=b_ps[:, 1, 0:12])
+
+        hx_c = keep.tile([P, 1024], U32, name="hx_c", align_bytes=64)
+        hx_s = keep.tile([P, 1024], U8, name="hx_s", align_bytes=64)
+        w1_c = keep.tile([P, 1536], U32, name="w1_c", align_bytes=64)
+        w1_s = keep.tile([P, 1536], U8, name="w1_s", align_bytes=64)
+        w2_c = keep.tile([P, 1536], U32, name="w2_c", align_bytes=64)
+        w2_s = keep.tile([P, 1536], U8, name="w2_s", align_bytes=64)
+
+        def prep(src_words, codes, scales, engines):
+            grouped = stage.tile([P, 2048], BF16, name="grouped", tag="grouped", align_bytes=64)
+            g_words = grouped[:].bitcast(F32)
+            for bk in range(2):
+                xt = psum_tp.tile([P, 2, 256], F32, name="xt", tag="tp")
+                for i in range(2):
+                    for u in range(2):
+                        w0 = (2 * bk + i) * 256 + u * P
+                        nc.tensor.transpose(xt[:, u, i * P:(i + 1) * P], src_words[:, w0:w0 + P], ident[:])
+                dst = g_words[:, bk * 512:(bk + 1) * 512].rearrange("q (c u) -> q c u", u=2)
+                src = xt[:].rearrange("q u c -> q c u")
+                if engines[bk] == "v":
+                    nc.vector.tensor_copy(out=dst, in_=src)
+                else:
+                    nc.scalar.copy(out=dst, in_=src)
+            nc.vector.quantize_mx(out=codes.bitcast(FP8X4), scales=scales, in_=grouped[:])
+
+        def prep_hx(c, engines):
+            cols = slice(c * 512, (c + 1) * 512)
+            prep(hx_sb[:].bitcast(F32)[:, c * 1024:(c + 1) * 1024], hx_c[:, cols], hx_s[:, cols], engines)
+
+        def prep_w1(g, engines):
+            cols = slice(g * 512, (g + 1) * 512)
+            prep(w1_sb[g][:].bitcast(F32), w1_c[:, cols], w1_s[:, cols], engines)
+
+        def prep_w2(g, engines):
+            cols = slice(g * 512, (g + 1) * 512)
+            prep(w2_sb[g][:].bitcast(F32), w2_c[:, cols], w2_s[:, cols], engines)
+
+        a1_c = {}
+        a1_s = {}
+        gate = {}
+
+        def layer1(g, c):
+            planes = stage.tile([P, 4, 512], BF16, name="planes", tag="planes")
+            for t in range(4):
+                ps = psum_mm.tile([P, 512], F32, name="ps1", tag="mm")
+                col = g * 512 + t * P
+                nc.tensor.matmul_mx(
+                    out=ps[:],
+                    lhsT=w1_c[:, col:col + P].bitcast(FP8X4),
+                    lhsT_scale=w1_s[:, col:col + P],
+                    rhs=hx_c[:, c * 512:(c + 1) * 512].bitcast(FP8X4),
+                    rhs_scale=hx_s[:, c * 512:(c + 1) * 512],
+                    start=True,
+                    stop=True,
+                )
+                nc.scalar.activation(out=planes[:, t, :], in_=ps[:], func=ACT.Tanh,
+                                     bias=bias1[:, g * 4 + t:g * 4 + t + 1], scale=1.0)
+            a1_g = stage.tile([P, 512, 4], BF16, name="a1_g", tag="a1_g", align_bytes=64)
+            nc.vector.tensor_copy(
+                out=a1_g[:].rearrange("p (c i) t -> p c t i", i=4),
+                in_=planes[:].rearrange("p t (c i) -> p c t i", i=4),
+            )
+            a1_c[(g, c)] = keep.tile([P, 512], U32, name="a1_c%d%d" % (g, c), align_bytes=64)
+            a1_s[(g, c)] = keep.tile([P, 512], U8, name="a1_s%d%d" % (g, c), align_bytes=64)
+            nc.vector.quantize_mx(
+                out=a1_c[(g, c)][:].bitcast(FP8X4),
+                scales=a1_s[(g, c)][:],
+                in_=a1_g[:].rearrange("p b t -> p (b t)"),
+            )
+
+        def layer2(g, c):
+            gt = keep.tile([P, 4, 512], F32, name="gate%d%d" % (g, c))
+            gate[(g, c)] = gt
+            for t in range(4):
+                ps = psum_mm.tile([P, 512], F32, name="ps2", tag="mm")
+                col = g * 512 + t * P
+                nc.tensor.matmul_mx(
+                    out=ps[:],
+                    lhsT=w2_c[:, col:col + P].bitcast(FP8X4),
+                    lhsT_scale=w2_s[:, col:col + P],
+                    rhs=a1_c[(g, c)][:].bitcast(FP8X4),
+                    rhs_scale=a1_s[(g, c)][:],
+                    start=True,
+                    stop=True,
+                )
+                nc.scalar.activation(out=gt[:, t, :], in_=ps[:], func=ACT.Tanh,
+                                     bias=bias2[:, g * 4 + t:g * 4 + t + 1], scale=1.0)
+
+        def half_tanh(g, c, cols):
+            view = gate[(g, c)][:, :, cols]
+            nc.scalar.activation(out=view, in_=view, func=ACT.Tanh, scale=0.5)
+
+        def candidate(c):
+            view = gate[(2, c)][:, :, :]
+            nc.scalar.activation(out=view, in_=view, func=ACT.Tanh, bias=0.5, scale=0.5)
+
+        forget = {}
+        out_rows = out.rearrange("(p j) h -> p j h", j=8)
+
+        def back(src, jl):
+            ps = psum_tp.tile([P, 512], F32, name="back", tag="tp")
+            for t in range(4):
+                nc.tensor.transpose(ps[:, t * P:(t + 1) * P], src[:, t, jl * P:(jl + 1) * P], ident[:])
+            return ps
+
+        def forget_part(c, jl):
+            j = 4 * c + jl
+            ps = back(gate[(1, c)], jl)
+            fg = outp.tile([P, 512], F32, name="fg", tag="fg")
+            forget[j] = fg
+            nc.vector.scalar_tensor_tensor(out=fg[:], in0=ps[:], scalar=1.0, in1=cx_sb[:, j * 512:(j + 1) * 512],
+                                           op0=ALU.add, op1=ALU.mult)
+
+        def input_part(c, jl):
+            j = 4 * c + jl
+            cols = slice(jl * P, (jl + 1) * P)
+            iv = gate[(0, c)][:, :, cols]
+            nc.vector.scalar_tensor_tensor(out=iv, in0=iv, scalar=1.0, in1=gate[(2, c)][:, :, cols],
+                                           op0=ALU.add, op1=ALU.mult)
+            ps = back(gate[(0, c)], jl)
+            res = outp.tile([P, 512], F32, name="res", tag="res")
+            nc.vector.scalar_tensor_tensor(out=res[:], in0=ps[:], scalar=0.5, in1=forget[j][:],
+                                           op0=ALU.mult, op1=ALU.add)
+            nc.sync.dma_start(out=out_rows[:, j, :], in_=res[:])
+
+        full = slice(0, 512)
+        prep_hx(0, "va")
+        prep_w1(1, "av")
+        layer1(1, 0)
+        prep_w1(2, "vv")
+        layer1(2, 0)
+        prep_w1(0, "vv")
+        layer1(0, 0)
+        prep_w2(1, "vv")
+        layer2(1, 0)
+        half_tanh(1, 0, full)
+        prep_w2(2, "vv")
+        layer2(2, 0)
+        half_tanh(2, 0, full)
+        candidate(0)
+        prep_w2(0, "vv")
+        layer2(0, 0)
+        prep_hx(1, "vv")
+        nc.vector.tensor_scalar_mul(out=cx_sb[:], in0=cx_sb[:], scalar1=0.5)
+        for jl in range(4):
+            half_tanh(0, 0, slice(jl * P, (jl + 1) * P))
+        layer1(1, 1)
+        layer1(2, 1)
+        layer1(0, 1)
+        for jl in range(4):
+            forget_part(0, jl)
+        for jl in range(4):
+            input_part(0, jl)
+        layer2(1, 1)
+        half_tanh(1, 1, full)
+        layer2(2, 1)
+        for jl in range(4):
+            forget_part(1, jl)
+        half_tanh(2, 1, full)
+        candidate(1)
+        layer2(0, 1)
+        for jl in range(4):
+            half_tanh(0, 1, slice(jl * P, (jl + 1) * P))
+            input_part(1, jl)

@@ -14,235 +14,423 @@ ACT = mybir.ActivationFunctionType
 ALU = mybir.AluOpType
 
 P = 128
-GATE_ORDER = (1, 2, 0)
+ALL = slice(0, 512)
+LOW = slice(0, 2)
+HIGH = slice(2, 4)
+BOTH = slice(0, 4)
+
+
+def blk(jl):
+    return slice(jl * P, (jl + 1) * P)
 
 
 def tile_lstmcellunknowndata_pa_kernel(tc, hx, cx2, w1, b1, w2, b2, out):
     nc = tc.nc
     with ExitStack() as ctx:
         keep = ctx.enter_context(tc.tile_pool(name="keep", bufs=1))
-        stage = ctx.enter_context(tc.tile_pool(name="stage", bufs=3))
+        stage = ctx.enter_context(tc.tile_pool(name="stage", bufs=4))
+        plane_pool = ctx.enter_context(tc.tile_pool(name="plane_pool", bufs=6))
+        f_pool = ctx.enter_context(tc.tile_pool(name="f_pool", bufs=8))
         outp = ctx.enter_context(tc.tile_pool(name="outp", bufs=4))
         psum_mm = ctx.enter_context(tc.psum_pool(name="psmm", bufs=4))
-        psum_tp = ctx.enter_context(tc.psum_pool(name="pstp", bufs=4))
+        psum_tp = ctx.enter_context(tc.psum_pool(name="pstp", bufs=8 - 4))
+        ctx.enter_context(tc.manual_schedule())
+        hx_sb = keep.tile([P, 4096], BF16, name="hx_sb")
+        cx_sb = keep.tile([P, 4096], BF16, name="cx_sb")
+        hx_c = keep.tile([P, 1024], U32, name="hx_c", align_bytes=64)
+        hx_s = keep.tile([P, 1024], U8, name="hx_s", align_bytes=64)
+        raw = {}
+        words = {}
+        codes = {}
+        scales = {}
+        for c in range(2):
+            raw["hx%d" % c] = hx_sb[:, c * 2048:(c + 1) * 2048]
+            words["hx%d" % c] = hx_sb[:].bitcast(F32)[:, c * 1024:(c + 1) * 1024]
+            codes["hx%d" % c] = hx_c[:, c * 512:(c + 1) * 512]
+            scales["hx%d" % c] = hx_s[:, c * 512:(c + 1) * 512]
+        for layer in (1, 2):
+            for g in range(3):
+                x = "w%d_%d" % (layer, g)
+                w_sb = keep.tile([P, 2048], BF16, name="sb_" + x)
+                w_c = keep.tile([P, 512], U32, name="c_" + x, align_bytes=64)
+                w_s = keep.tile([P, 512], U8, name="s_" + x, align_bytes=64)
+                raw[x] = w_sb[:]
+                words[x] = w_sb[:].bitcast(F32)
+                codes[x] = w_c[:]
+                scales[x] = w_s[:]
+        hx_rows = hx.rearrange("(p j) k -> p (j k)", j=8)
+        dram = {}
+        for c in range(2):
+            dram["hx%d" % c] = hx_rows[:, c * 2048:(c + 1) * 2048].rearrange("p (b x) -> p b x", b=2)
+        for g in range(3):
+            dram["w1_%d" % g] = w1[g].rearrange("(u p e) k -> p u (e k)", u=2, e=2)
+            dram["w2_%d" % g] = w2[g].rearrange("(b t p) f -> p b t f", b=2, p=P)
+
+        def load(x, bk):
+            if bk is None:
+                if x[0:2] == "w2":
+                    nc.sync.dma_start(out=raw[x].rearrange("p (t f) -> p t f", t=4),
+                                      in_=dram[x].rearrange("p b t f -> p (b t) f"))
+                else:
+                    nc.sync.dma_start(out=raw[x].rearrange("p (b x) -> p b x", b=2), in_=dram[x])
+            elif x[0:2] == "w2":
+                nc.sync.dma_start(out=raw[x][:, bk * 1024:(bk + 1) * 1024].rearrange("p (t f) -> p t f", t=2),
+                                  in_=dram[x][:, bk, :, :])
+            else:
+                nc.sync.dma_start(out=raw[x][:, bk * 1024:(bk + 1) * 1024], in_=dram[x][:, bk, :])
 
         b1_raw = keep.tile([P, 256], BF16, name="b1_raw")
         b2_raw = keep.tile([P, P], BF16, name="b2_raw")
-        nc.vector.memset(b1_raw[:], 0.0)
-        nc.vector.memset(b2_raw[:], 0.0)
-        nc.scalar.dma_start(out=b1_raw[0:6, :], in_=b1.rearrange("g (u x) -> (g u) x", u=2))
-        nc.scalar.dma_start(out=b2_raw[0:12, :], in_=b2.rearrange("g (t x) -> (g t) x", t=4))
-        hx_sb = keep.tile([P, 4096], BF16, name="hx_sb")
-        cx_sb = keep.tile([P, 4096], BF16, name="cx_sb")
-        w1_sb = {}
-        w2_sb = {}
-        for g in range(3):
-            w1_sb[g] = keep.tile([P, 2048], BF16, name="w1_sb%d" % g)
-            w2_sb[g] = keep.tile([P, 2048], BF16, name="w2_sb%d" % g)
-        hx_rows = hx.rearrange("(p j) k -> p (j k)", j=8)
-
-        def load_w1(g):
-            nc.sync.dma_start(
-                out=w1_sb[g][:].rearrange("p (u x) -> p u x", u=2),
-                in_=w1[g].rearrange("(u p e) k -> p u (e k)", u=2, e=2),
-            )
-
-        def load_w2(g):
-            nc.sync.dma_start(
-                out=w2_sb[g][:].rearrange("p (t f) -> p t f", t=4),
-                in_=w2[g].rearrange("(t p) f -> p t f", p=P),
-            )
-
-        nc.sync.dma_start(out=hx_sb[:, 0:2048], in_=hx_rows[:, 0:2048])
-        load_w1(GATE_ORDER[0])
-        load_w1(GATE_ORDER[1])
-        load_w1(GATE_ORDER[2])
-        load_w2(GATE_ORDER[0])
-        load_w2(GATE_ORDER[1])
-        load_w2(GATE_ORDER[2])
-        nc.sync.dma_start(out=hx_sb[:, 2048:4096], in_=hx_rows[:, 2048:4096])
-        nc.sync.dma_start(out=cx_sb[:], in_=cx2.rearrange("(p j) h -> p (j h)", j=8))
-
+        b2_f32 = keep.tile([P, P], F32, name="b2_f32")
+        b1_words = keep.tile([P, 8], F32, name="b1_words")
+        bias = {1: keep.tile([P, 12], F32, name="bias1"), 2: keep.tile([P, 12], F32, name="bias2")}
         warm_in = keep.tile([P, 1], F32, name="warm_in")
         warm_out = keep.tile([P, 1], F32, name="warm_out")
-        nc.vector.memset(warm_in[:], 0.0)
-        nc.scalar.activation(out=warm_out[:], in_=warm_in[:], func=ACT.Tanh)
-
         ident = keep.tile([P, P], F32, name="ident")
+
+        nc.vector.memset(b1_raw[:], 0.0)
+        nc.vector.memset(b2_raw[:], 0.0)
+        nc.vector.memset(warm_in[:], 0.0)
+        nc.scalar.dma_start(out=b1_raw[0:6, :], in_=b1.rearrange("g (u x) -> (g u) x", u=2))
+        nc.scalar.dma_start(out=b2_raw[0:12, :], in_=b2.rearrange("g (t x) -> (g t) x", t=4))
+        nc.scalar.activation(out=warm_out[:], in_=warm_in[:], func=ACT.Tanh)
         make_identity(nc, ident[:])
+        load("w1_1", 0)
+        load("hx0", 0)
+        load("hx0", 1)
+        load("w1_1", 1)
+        load("w1_2", None)
+        load("w1_0", None)
+        load("hx1", None)
+        load("w2_1", None)
+        load("w2_2", None)
+        load("w2_0", None)
+        nc.sync.dma_start(out=cx_sb[:], in_=cx2.rearrange("(p j) h -> p (j h)", j=8))
+        live = {}
 
-        b2_f32 = keep.tile([P, P], F32, name="b2_f32")
-        nc.vector.tensor_copy(out=b2_f32[:], in_=b2_raw[:])
-        b_ps = psum_tp.tile([P, 2, P], F32, name="b_ps", tag="tp")
-        nc.tensor.transpose(b_ps[:, 0, :], b1_raw[:].bitcast(F32), ident[:])
-        nc.tensor.transpose(b_ps[:, 1, :], b2_f32[:], ident[:])
-        b1_words = keep.tile([P, 8], F32, name="b1_words")
-        nc.vector.tensor_copy(out=b1_words[:, 0:6], in_=b_ps[:, 0, 0:6])
-        bias1 = keep.tile([P, 12], F32, name="bias1")
-        nc.vector.tensor_copy(out=bias1[:], in_=b1_words[:, 0:6].bitcast(BF16))
-        bias2 = keep.tile([P, 12], F32, name="bias2")
-        nc.vector.tensor_copy(out=bias2[:], in_=b_ps[:, 1, 0:12])
+        def bias_cast():
+            nc.vector.tensor_copy(out=b2_f32[:], in_=b2_raw[:])
 
-        hx_c = keep.tile([P, 1024], U32, name="hx_c", align_bytes=64)
-        hx_s = keep.tile([P, 1024], U8, name="hx_s", align_bytes=64)
-        w1_c = keep.tile([P, 1536], U32, name="w1_c", align_bytes=64)
-        w1_s = keep.tile([P, 1536], U8, name="w1_s", align_bytes=64)
-        w2_c = keep.tile([P, 1536], U32, name="w2_c", align_bytes=64)
-        w2_s = keep.tile([P, 1536], U8, name="w2_s", align_bytes=64)
+        def bias_tr():
+            b_ps = psum_tp.tile([P, 2, P], F32, name="b_ps", tag="tp")
+            live["b_ps"] = b_ps
+            nc.tensor.transpose(b_ps[:, 0, :], b1_raw[:].bitcast(F32), ident[:])
+            nc.tensor.transpose(b_ps[:, 1, :], b2_f32[:], ident[:])
 
-        def prep(src_words, codes, scales, engines):
-            grouped = stage.tile([P, 2048], BF16, name="grouped", tag="grouped", align_bytes=64)
-            g_words = grouped[:].bitcast(F32)
-            for bk in range(2):
-                xt = psum_tp.tile([P, 2, 256], F32, name="xt", tag="tp")
-                for i in range(2):
-                    for u in range(2):
-                        w0 = (2 * bk + i) * 256 + u * P
-                        nc.tensor.transpose(xt[:, u, i * P:(i + 1) * P], src_words[:, w0:w0 + P], ident[:])
-                dst = g_words[:, bk * 512:(bk + 1) * 512].rearrange("q (c u) -> q c u", u=2)
-                src = xt[:].rearrange("q u c -> q c u")
-                if engines[bk] == "v":
-                    nc.vector.tensor_copy(out=dst, in_=src)
-                else:
-                    nc.scalar.copy(out=dst, in_=src)
-            nc.vector.quantize_mx(out=codes.bitcast(FP8X4), scales=scales, in_=grouped[:])
+        def bias_out():
+            b_ps = live["b_ps"]
+            nc.vector.tensor_copy(out=b1_words[:, 0:6], in_=b_ps[:, 0, 0:6])
+            nc.vector.tensor_copy(out=bias[2][:], in_=b_ps[:, 1, 0:12])
+            nc.vector.tensor_copy(out=bias[1][:], in_=b1_words[:, 0:6].bitcast(BF16))
 
-        def prep_hx(c, engines):
-            cols = slice(c * 512, (c + 1) * 512)
-            prep(hx_sb[:].bitcast(F32)[:, c * 1024:(c + 1) * 1024], hx_c[:, cols], hx_s[:, cols], engines)
+        def tr(x, bk):
+            xt = psum_tp.tile([P, 2, 256], F32, name="xt", tag="tp")
+            live[("xt", x, bk)] = xt
+            for i in range(2):
+                for u in range(2):
+                    w0 = (2 * bk + i) * 256 + u * P
+                    nc.tensor.transpose(xt[:, u, i * P:(i + 1) * P], words[x][:, w0:w0 + P], ident[:])
 
-        def prep_w1(g, engines):
-            cols = slice(g * 512, (g + 1) * 512)
-            prep(w1_sb[g][:].bitcast(F32), w1_c[:, cols], w1_s[:, cols], engines)
+        def ev(x, bk, copy):
+            if ("grouped", x) not in live:
+                live[("grouped", x)] = stage.tile([P, 2048], BF16, name="grouped", tag="grouped", align_bytes=64)
+            g_words = live[("grouped", x)][:].bitcast(F32)
+            copy(out=g_words[:, bk * 512:(bk + 1) * 512].rearrange("q (c u) -> q c u", u=2),
+                 in_=live[("xt", x, bk)][:].rearrange("q u c -> q c u"))
 
-        def prep_w2(g, engines):
-            cols = slice(g * 512, (g + 1) * 512)
-            prep(w2_sb[g][:].bitcast(F32), w2_c[:, cols], w2_s[:, cols], engines)
+        def qx(x, bk):
+            nc.vector.quantize_mx(out=codes[x][:, bk * 256:(bk + 1) * 256].bitcast(FP8X4),
+                                  scales=scales[x][:, bk * 256:(bk + 1) * 256],
+                                  in_=live[("grouped", x)][:, bk * 1024:(bk + 1) * 1024])
 
-        a1_c = {}
-        a1_s = {}
-        gate = {}
+        def mm(layer, g, c, t):
+            ps = psum_mm.tile([P, 512], F32, name="ps", tag="mm")
+            live[("ps", layer, g, c, t)] = ps
+            x = "w%d_%d" % (layer, g)
+            if layer == 1:
+                rhs, rhs_scale = codes["hx%d" % c], scales["hx%d" % c]
+            else:
+                rhs, rhs_scale = live[("a1_c", g, c)][:], live[("a1_s", g, c)][:]
+            nc.tensor.matmul_mx(out=ps[:], lhsT=codes[x][:, t * P:(t + 1) * P].bitcast(FP8X4),
+                                lhsT_scale=scales[x][:, t * P:(t + 1) * P],
+                                rhs=rhs.bitcast(FP8X4), rhs_scale=rhs_scale, start=True, stop=True)
 
-        def layer1(g, c):
-            planes = stage.tile([P, 4, 512], BF16, name="planes", tag="planes")
-            for t in range(4):
-                ps = psum_mm.tile([P, 512], F32, name="ps1", tag="mm")
-                col = g * 512 + t * P
-                nc.tensor.matmul_mx(
-                    out=ps[:],
-                    lhsT=w1_c[:, col:col + P].bitcast(FP8X4),
-                    lhsT_scale=w1_s[:, col:col + P],
-                    rhs=hx_c[:, c * 512:(c + 1) * 512].bitcast(FP8X4),
-                    rhs_scale=hx_s[:, c * 512:(c + 1) * 512],
-                    start=True,
-                    stop=True,
-                )
-                nc.scalar.activation(out=planes[:, t, :], in_=ps[:], func=ACT.Tanh,
-                                     bias=bias1[:, g * 4 + t:g * 4 + t + 1], scale=1.0)
+        def th(layer, g, c, t):
+            if layer == 1:
+                if t == 0:
+                    live[("planes", g, c)] = plane_pool.tile([P, 4, 512], BF16, name="planes", tag="planes")
+                dst = live[("planes", g, c)]
+            else:
+                if t == 0:
+                    live[("gate", g, c)] = keep.tile([P, 4, 512], F32, name="gate%d%d" % (g, c))
+                dst = live[("gate", g, c)]
+            nc.scalar.activation(out=dst[:, t, :], in_=live[("ps", layer, g, c, t)][:], func=ACT.Tanh,
+                                 bias=bias[layer][:, g * 4 + t:g * 4 + t + 1], scale=1.0)
+
+        def rg(g, c):
             a1_g = stage.tile([P, 512, 4], BF16, name="a1_g", tag="a1_g", align_bytes=64)
-            nc.vector.tensor_copy(
-                out=a1_g[:].rearrange("p (c i) t -> p c t i", i=4),
-                in_=planes[:].rearrange("p t (c i) -> p c t i", i=4),
-            )
-            a1_c[(g, c)] = keep.tile([P, 512], U32, name="a1_c%d%d" % (g, c), align_bytes=64)
-            a1_s[(g, c)] = keep.tile([P, 512], U8, name="a1_s%d%d" % (g, c), align_bytes=64)
-            nc.vector.quantize_mx(
-                out=a1_c[(g, c)][:].bitcast(FP8X4),
-                scales=a1_s[(g, c)][:],
-                in_=a1_g[:].rearrange("p b t -> p (b t)"),
-            )
+            live[("a1_g", g, c)] = a1_g
+            nc.vector.tensor_copy(out=a1_g[:].rearrange("p (c i) t -> p c t i", i=4),
+                                  in_=live[("planes", g, c)][:].rearrange("p t (c i) -> p c t i", i=4))
 
-        def layer2(g, c):
-            gt = keep.tile([P, 4, 512], F32, name="gate%d%d" % (g, c))
-            gate[(g, c)] = gt
-            for t in range(4):
-                ps = psum_mm.tile([P, 512], F32, name="ps2", tag="mm")
-                col = g * 512 + t * P
-                nc.tensor.matmul_mx(
-                    out=ps[:],
-                    lhsT=w2_c[:, col:col + P].bitcast(FP8X4),
-                    lhsT_scale=w2_s[:, col:col + P],
-                    rhs=a1_c[(g, c)][:].bitcast(FP8X4),
-                    rhs_scale=a1_s[(g, c)][:],
-                    start=True,
-                    stop=True,
-                )
-                nc.scalar.activation(out=gt[:, t, :], in_=ps[:], func=ACT.Tanh,
-                                     bias=bias2[:, g * 4 + t:g * 4 + t + 1], scale=1.0)
+        def qa(g, c):
+            live[("a1_c", g, c)] = keep.tile([P, 512], U32, name="a1_c%d%d" % (g, c), align_bytes=64)
+            live[("a1_s", g, c)] = keep.tile([P, 512], U8, name="a1_s%d%d" % (g, c), align_bytes=64)
+            nc.vector.quantize_mx(out=live[("a1_c", g, c)][:].bitcast(FP8X4), scales=live[("a1_s", g, c)][:],
+                                  in_=live[("a1_g", g, c)][:].rearrange("p b t -> p (b t)"))
 
-        def half_tanh(g, c, cols):
-            view = gate[(g, c)][:, :, cols]
+        def sg(g, c, rows, cols):
+            view = live[("gate", g, c)][:, rows, cols]
             nc.scalar.activation(out=view, in_=view, func=ACT.Tanh, scale=0.5)
 
-        def candidate(c):
-            view = gate[(2, c)][:, :, :]
+        def zc(c, rows, cols):
+            view = live[("gate", 2, c)][:, rows, cols]
             nc.scalar.activation(out=view, in_=view, func=ACT.Tanh, bias=0.5, scale=0.5)
 
-        forget = {}
+        def cxh():
+            nc.vector.tensor_scalar_mul(out=cx_sb[:], in0=cx_sb[:], scalar1=0.5)
+
+        def bk(g, c, jl):
+            ps = psum_tp.tile([P, 512], F32, name="back", tag="tp")
+            live[("back", g, c, jl)] = ps
+            for t in range(4):
+                nc.tensor.transpose(ps[:, t * P:(t + 1) * P], live[("gate", g, c)][:, t, blk(jl)], ident[:])
+
+        def fg(c, jl):
+            j = 4 * c + jl
+            f_sb = f_pool.tile([P, 512], F32, name="f_sb", tag="f_sb")
+            live[("f_sb", j)] = f_sb
+            nc.vector.scalar_tensor_tensor(out=f_sb[:], in0=live[("back", 1, c, jl)][:], scalar=1.0,
+                                           in1=cx_sb[:, j * 512:(j + 1) * 512], op0=ALU.add, op1=ALU.mult)
+
+        def pi(c, cols):
+            view = live[("gate", 0, c)][:, :, cols]
+            nc.vector.scalar_tensor_tensor(out=view, in0=view, scalar=1.0, in1=live[("gate", 2, c)][:, :, cols],
+                                           op0=ALU.add, op1=ALU.mult)
+
         out_rows = out.rearrange("(p j) h -> p j h", j=8)
 
-        def back(src, jl):
-            ps = psum_tp.tile([P, 512], F32, name="back", tag="tp")
-            for t in range(4):
-                nc.tensor.transpose(ps[:, t * P:(t + 1) * P], src[:, t, jl * P:(jl + 1) * P], ident[:])
-            return ps
-
-        def forget_part(c, jl):
+        def res(c, jl):
             j = 4 * c + jl
-            ps = back(gate[(1, c)], jl)
-            fg = outp.tile([P, 512], F32, name="fg", tag="fg")
-            forget[j] = fg
-            nc.vector.scalar_tensor_tensor(out=fg[:], in0=ps[:], scalar=1.0, in1=cx_sb[:, j * 512:(j + 1) * 512],
-                                           op0=ALU.add, op1=ALU.mult)
+            r_sb = outp.tile([P, 512], F32, name="r_sb", tag="r_sb")
+            nc.vector.scalar_tensor_tensor(out=r_sb[:], in0=live[("back", 0, c, jl)][:], scalar=0.5,
+                                           in1=live[("f_sb", j)][:], op0=ALU.mult, op1=ALU.add)
+            nc.sync.dma_start(out=out_rows[:, j, :], in_=r_sb[:])
 
-        def input_part(c, jl):
-            j = 4 * c + jl
-            cols = slice(jl * P, (jl + 1) * P)
-            iv = gate[(0, c)][:, :, cols]
-            nc.vector.scalar_tensor_tensor(out=iv, in0=iv, scalar=1.0, in1=gate[(2, c)][:, :, cols],
-                                           op0=ALU.add, op1=ALU.mult)
-            ps = back(gate[(0, c)], jl)
-            res = outp.tile([P, 512], F32, name="res", tag="res")
-            nc.vector.scalar_tensor_tensor(out=res[:], in0=ps[:], scalar=0.5, in1=forget[j][:],
-                                           op0=ALU.mult, op1=ALU.add)
-            nc.sync.dma_start(out=out_rows[:, j, :], in_=res[:])
-
-        full = slice(0, 512)
-        prep_hx(0, "va")
-        prep_w1(1, "av")
-        layer1(1, 0)
-        prep_w1(2, "vv")
-        layer1(2, 0)
-        prep_w1(0, "vv")
-        layer1(0, 0)
-        prep_w2(1, "vv")
-        layer2(1, 0)
-        half_tanh(1, 0, full)
-        prep_w2(2, "vv")
-        layer2(2, 0)
-        half_tanh(2, 0, full)
-        candidate(0)
-        prep_w2(0, "vv")
-        layer2(0, 0)
-        prep_hx(1, "vv")
-        nc.vector.tensor_scalar_mul(out=cx_sb[:], in0=cx_sb[:], scalar1=0.5)
-        for jl in range(4):
-            half_tanh(0, 0, slice(jl * P, (jl + 1) * P))
-        layer1(1, 1)
-        layer1(2, 1)
-        layer1(0, 1)
-        for jl in range(4):
-            forget_part(0, jl)
-        for jl in range(4):
-            input_part(0, jl)
-        layer2(1, 1)
-        half_tanh(1, 1, full)
-        layer2(2, 1)
-        for jl in range(4):
-            forget_part(1, jl)
-        half_tanh(2, 1, full)
-        candidate(1)
-        layer2(0, 1)
-        for jl in range(4):
-            half_tanh(0, 1, slice(jl * P, (jl + 1) * P))
-            input_part(1, jl)
+        tr("w1_1", 0)
+        ev("w1_1", 0, nc.scalar.copy)
+        tr("hx0", 0)
+        ev("hx0", 0, nc.vector.tensor_copy)
+        tr("hx0", 1)
+        qx("w1_1", 0)
+        ev("hx0", 1, nc.scalar.copy)
+        tr("w1_1", 1)
+        qx("hx0", 0)
+        bias_cast()
+        ev("w1_1", 1, nc.scalar.copy)
+        qx("hx0", 1)
+        bias_tr()
+        tr("w1_2", 0)
+        qx("w1_1", 1)
+        tr("w1_2", 1)
+        bias_out()
+        mm(1, 1, 0, 0)
+        ev("w1_2", 0, nc.vector.tensor_copy)
+        mm(1, 1, 0, 1)
+        th(1, 1, 0, 0)
+        ev("w1_2", 1, nc.vector.tensor_copy)
+        mm(1, 1, 0, 2)
+        mm(1, 1, 0, 3)
+        th(1, 1, 0, 1)
+        qx("w1_2", 0)
+        tr("w1_0", 0)
+        qx("w1_2", 1)
+        tr("w1_0", 1)
+        th(1, 1, 0, 2)
+        ev("w1_0", 0, nc.vector.tensor_copy)
+        mm(1, 2, 0, 0)
+        th(1, 1, 0, 3)
+        mm(1, 2, 0, 1)
+        ev("w1_0", 1, nc.vector.tensor_copy)
+        mm(1, 2, 0, 2)
+        th(1, 2, 0, 0)
+        qx("w1_0", 0)
+        mm(1, 2, 0, 3)
+        qx("w1_0", 1)
+        tr("hx1", 0)
+        th(1, 2, 0, 1)
+        tr("hx1", 1)
+        ev("hx1", 0, nc.vector.tensor_copy)
+        th(1, 2, 0, 2)
+        mm(1, 0, 0, 0)
+        mm(1, 0, 0, 1)
+        ev("hx1", 1, nc.vector.tensor_copy)
+        th(1, 2, 0, 3)
+        mm(1, 0, 0, 2)
+        qx("hx1", 0)
+        th(1, 0, 0, 0)
+        mm(1, 0, 0, 3)
+        qx("hx1", 1)
+        tr("w2_1", 0)
+        rg(1, 0)
+        th(1, 0, 0, 1)
+        tr("w2_1", 1)
+        th(1, 0, 0, 2)
+        mm(1, 1, 1, 0)
+        mm(1, 1, 1, 1)
+        th(1, 0, 0, 3)
+        ev("w2_1", 0, nc.vector.tensor_copy)
+        mm(1, 1, 1, 2)
+        qa(1, 0)
+        th(1, 1, 1, 0)
+        mm(1, 1, 1, 3)
+        tr("w2_2", 0)
+        th(1, 1, 1, 1)
+        ev("w2_1", 1, nc.vector.tensor_copy)
+        tr("w2_2", 1)
+        th(1, 1, 1, 2)
+        qx("w2_1", 0)
+        mm(1, 2, 1, 0)
+        qx("w2_1", 1)
+        mm(1, 2, 1, 1)
+        th(1, 1, 1, 3)
+        mm(1, 2, 1, 2)
+        th(1, 2, 1, 0)
+        mm(1, 2, 1, 3)
+        rg(1, 1)
+        tr("w2_0", 0)
+        th(1, 2, 1, 1)
+        tr("w2_0", 1)
+        th(1, 2, 1, 2)
+        mm(1, 0, 1, 0)
+        ev("w2_2", 0, nc.vector.tensor_copy)
+        mm(1, 0, 1, 1)
+        th(1, 2, 1, 3)
+        qa(1, 1)
+        mm(1, 0, 1, 2)
+        th(1, 0, 1, 0)
+        mm(1, 0, 1, 3)
+        ev("w2_2", 1, nc.vector.tensor_copy)
+        th(1, 0, 1, 1)
+        mm(2, 1, 0, 0)
+        qx("w2_2", 0)
+        qx("w2_2", 1)
+        th(1, 0, 1, 2)
+        mm(2, 1, 0, 1)
+        rg(2, 0)
+        th(1, 0, 1, 3)
+        mm(2, 1, 0, 2)
+        th(2, 1, 0, 0)
+        mm(2, 1, 0, 3)
+        ev("w2_0", 0, nc.vector.tensor_copy)
+        th(2, 1, 0, 1)
+        mm(2, 1, 1, 0)
+        qa(2, 0)
+        th(2, 1, 0, 2)
+        mm(2, 1, 1, 1)
+        ev("w2_0", 1, nc.vector.tensor_copy)
+        th(2, 1, 0, 3)
+        mm(2, 1, 1, 2)
+        qx("w2_0", 0)
+        sg(1, 0, LOW, ALL)
+        qx("w2_0", 1)
+        mm(2, 1, 1, 3)
+        rg(0, 0)
+        sg(1, 0, HIGH, ALL)
+        cxh()
+        th(2, 1, 1, 0)
+        bk(1, 0, 0)
+        qa(0, 0)
+        th(2, 1, 1, 1)
+        bk(1, 0, 1)
+        rg(2, 1)
+        bk(1, 0, 2)
+        th(2, 1, 1, 2)
+        bk(1, 0, 3)
+        mm(2, 2, 0, 0)
+        th(2, 1, 1, 3)
+        mm(2, 2, 0, 1)
+        fg(0, 0)
+        sg(1, 1, LOW, ALL)
+        mm(2, 2, 0, 2)
+        mm(2, 2, 0, 3)
+        qa(2, 1)
+        rg(0, 1)
+        sg(1, 1, HIGH, ALL)
+        fg(0, 1)
+        th(2, 2, 0, 0)
+        bk(1, 1, 0)
+        qa(0, 1)
+        th(2, 2, 0, 1)
+        bk(1, 1, 1)
+        fg(0, 2)
+        th(2, 2, 0, 2)
+        fg(0, 3)
+        th(2, 2, 0, 3)
+        bk(1, 1, 2)
+        fg(1, 0)
+        sg(2, 0, LOW, ALL)
+        bk(1, 1, 3)
+        mm(2, 0, 0, 0)
+        fg(1, 1)
+        mm(2, 0, 0, 1)
+        fg(1, 2)
+        sg(2, 0, HIGH, ALL)
+        mm(2, 0, 0, 2)
+        mm(2, 0, 0, 3)
+        fg(1, 3)
+        zc(0, LOW, ALL)
+        zc(0, HIGH, ALL)
+        th(2, 0, 0, 0)
+        th(2, 0, 0, 1)
+        mm(2, 2, 1, 0)
+        th(2, 0, 0, 2)
+        mm(2, 2, 1, 1)
+        th(2, 0, 0, 3)
+        mm(2, 2, 1, 2)
+        sg(0, 0, LOW, ALL)
+        mm(2, 2, 1, 3)
+        sg(0, 0, HIGH, ALL)
+        th(2, 2, 1, 0)
+        pi(0, ALL)
+        th(2, 2, 1, 1)
+        mm(2, 0, 1, 0)
+        th(2, 2, 1, 2)
+        mm(2, 0, 1, 1)
+        th(2, 2, 1, 3)
+        mm(2, 0, 1, 2)
+        sg(2, 1, LOW, ALL)
+        mm(2, 0, 1, 3)
+        bk(0, 0, 0)
+        bk(0, 0, 1)
+        res(0, 0)
+        sg(2, 1, HIGH, ALL)
+        bk(0, 0, 2)
+        bk(0, 0, 3)
+        res(0, 1)
+        th(2, 0, 1, 0)
+        res(0, 2)
+        th(2, 0, 1, 1)
+        res(0, 3)
+        th(2, 0, 1, 2)
+        th(2, 0, 1, 3)
+        zc(1, BOTH, blk(0))
+        sg(0, 1, BOTH, blk(0))
+        zc(1, BOTH, blk(1))
+        pi(1, blk(0))
+        sg(0, 1, BOTH, blk(1))
+        bk(0, 1, 0)
+        zc(1, BOTH, blk(2))
+        pi(1, blk(1))
+        sg(0, 1, BOTH, blk(2))
+        res(1, 0)
+        bk(0, 1, 1)
+        zc(1, BOTH, blk(3))
+        pi(1, blk(2))
+        sg(0, 1, BOTH, blk(3))
+        res(1, 1)
+        bk(0, 1, 2)
+        pi(1, blk(3))
+        res(1, 2)
+        bk(0, 1, 3)
+        res(1, 3)

@@ -30,6 +30,7 @@ def tile_lstmcellunknowndata_pa_kernel(tc, hx, cx2, w1, b1, w2, b2, out):
         keep = ctx.enter_context(tc.tile_pool(name="keep", bufs=1))
         stage = ctx.enter_context(tc.tile_pool(name="stage", bufs=4))
         plane_pool = ctx.enter_context(tc.tile_pool(name="plane_pool", bufs=6))
+        t_pool = ctx.enter_context(tc.tile_pool(name="t_pool", bufs=4))
         f_pool = ctx.enter_context(tc.tile_pool(name="f_pool", bufs=8))
         outp = ctx.enter_context(tc.tile_pool(name="outp", bufs=4))
         psum_mm = ctx.enter_context(tc.psum_pool(name="psmm", bufs=4))
@@ -91,17 +92,20 @@ def tile_lstmcellunknowndata_pa_kernel(tc, hx, cx2, w1, b1, w2, b2, out):
         nc.vector.memset(b1_raw[:], 0.0)
         nc.vector.memset(b2_raw[:], 0.0)
         nc.vector.memset(warm_in[:], 0.0)
-        nc.scalar.dma_start(out=b1_raw[0:6, :], in_=b1.rearrange("g (u x) -> (g u) x", u=2))
-        nc.scalar.dma_start(out=b2_raw[0:12, :], in_=b2.rearrange("g (t x) -> (g t) x", t=4))
         nc.scalar.activation(out=warm_out[:], in_=warm_in[:], func=ACT.Tanh)
         make_identity(nc, ident[:])
         load("w1_1", 0)
         load("hx0", 0)
+        nc.sync.dma_start(out=b1_raw[0:6, :], in_=b1.rearrange("g (u x) -> (g u) x", u=2))
+        nc.sync.dma_start(out=b2_raw[0:12, :], in_=b2.rearrange("g (t x) -> (g t) x", t=4))
         load("hx0", 1)
         load("w1_1", 1)
-        load("w1_2", None)
-        load("w1_0", None)
-        load("hx1", None)
+        load("w1_2", 0)
+        load("w1_2", 1)
+        load("w1_0", 0)
+        load("w1_0", 1)
+        load("hx1", 0)
+        load("hx1", 1)
         load("w2_1", None)
         load("w2_2", None)
         load("w2_0", None)
@@ -109,7 +113,7 @@ def tile_lstmcellunknowndata_pa_kernel(tc, hx, cx2, w1, b1, w2, b2, out):
         live = {}
 
         def bias_cast():
-            nc.vector.tensor_copy(out=b2_f32[:], in_=b2_raw[:])
+            nc.gpsimd.tensor_copy(out=b2_f32[:], in_=b2_raw[:])
 
         def bias_tr():
             b_ps = psum_tp.tile([P, 2, P], F32, name="b_ps", tag="tp")
@@ -155,9 +159,26 @@ def tile_lstmcellunknowndata_pa_kernel(tc, hx, cx2, w1, b1, w2, b2, out):
                                 lhsT_scale=scales[x][:, t * P:(t + 1) * P],
                                 rhs=rhs.bitcast(FP8X4), rhs_scale=rhs_scale, start=True, stop=True)
 
+        def mm_half(g, c, t, half):
+            ps = psum_mm.tile([P, 256], F32, name="ps_half", tag="mm")
+            live[("ps_half", g, c, t, half)] = ps
+            x = "w1_%d" % g
+            cols = slice(half * 256, (half + 1) * 256)
+            nc.tensor.matmul_mx(out=ps[:], lhsT=codes[x][:, t * P:(t + 1) * P].bitcast(FP8X4),
+                                lhsT_scale=scales[x][:, t * P:(t + 1) * P],
+                                rhs=codes["hx%d" % c][:, cols].bitcast(FP8X4), rhs_scale=scales["hx%d" % c][:, cols],
+                                start=True, stop=True)
+
+        def th_half(g, c, t, half):
+            if ("planes", g, c) not in live:
+                live[("planes", g, c)] = plane_pool.tile([P, 4, 512], BF16, name="planes", tag="planes")
+            nc.scalar.activation(out=live[("planes", g, c)][:, t, half * 256:(half + 1) * 256],
+                                 in_=live[("ps_half", g, c, t, half)][:], func=ACT.Tanh,
+                                 bias=bias[1][:, g * 4 + t:g * 4 + t + 1], scale=1.0)
+
         def th(layer, g, c, t):
             if layer == 1:
-                if t == 0:
+                if ("planes", g, c) not in live:
                     live[("planes", g, c)] = plane_pool.tile([P, 4, 512], BF16, name="planes", tag="planes")
                 dst = live[("planes", g, c)]
             else:
@@ -217,169 +238,205 @@ def tile_lstmcellunknowndata_pa_kernel(tc, hx, cx2, w1, b1, w2, b2, out):
                                            in1=live[("f_sb", j)][:], op0=ALU.mult, op1=ALU.add)
             nc.sync.dma_start(out=out_rows[:, j, :], in_=r_sb[:])
 
+        def res_half(c, jl, half):
+            j = 4 * c + jl
+            cols = slice(half * 256, (half + 1) * 256)
+            r_sb = outp.tile([P, 256], F32, name="r_half", tag="r_half")
+            nc.vector.scalar_tensor_tensor(out=r_sb[:], in0=live[("back", 0, c, jl)][:, cols], scalar=0.5,
+                                           in1=live[("f_sb", j)][:, cols], op0=ALU.mult, op1=ALU.add)
+            nc.sync.dma_start(out=out_rows[:, j, cols], in_=r_sb[:])
+
+        def sg_back(jl, cols):
+            if ("t0", jl) not in live:
+                live[("t0", jl)] = t_pool.tile([P, 512], F32, name="t0", tag="t0")
+            nc.scalar.activation(out=live[("t0", jl)][:, cols], in_=live[("back", 0, 1, jl)][:, cols],
+                                 func=ACT.Tanh, scale=0.5)
+
+        def bk_z(jl):
+            ps = psum_mm.tile([P, 512], F32, name="z_back", tag="mm")
+            live[("z_back", jl)] = ps
+            for t in range(4):
+                nc.tensor.transpose(ps[:, t * P:(t + 1) * P], live[("gate", 2, 1)][:, t, blk(jl)], ident[:])
+
+        def pi_back(jl, cols):
+            view = live[("t0", jl)][:, cols]
+            nc.vector.scalar_tensor_tensor(out=view, in0=view, scalar=1.0, in1=live[("z_back", jl)][:, cols],
+                                           op0=ALU.add, op1=ALU.mult)
+
+        def res_back(jl, cols):
+            j = 4 + jl
+            r_sb = outp.tile([P, 512], F32, name="r_back", tag="r_sb")
+            nc.vector.scalar_tensor_tensor(out=r_sb[:, cols], in0=live[("t0", jl)][:, cols], scalar=0.5,
+                                           in1=live[("f_sb", j)][:, cols], op0=ALU.mult, op1=ALU.add)
+            nc.sync.dma_start(out=out_rows[:, j, cols], in_=r_sb[:, cols])
+
         tr("w1_1", 0)
         ev("w1_1", 0, nc.scalar.copy)
         tr("hx0", 0)
+        bias_cast()
         ev("hx0", 0, nc.vector.tensor_copy)
         tr("hx0", 1)
+        bias_tr()
         qx("w1_1", 0)
         ev("hx0", 1, nc.scalar.copy)
         tr("w1_1", 1)
         qx("hx0", 0)
-        bias_cast()
+        bias_out()
         ev("w1_1", 1, nc.scalar.copy)
-        qx("hx0", 1)
-        bias_tr()
         tr("w1_2", 0)
+        qx("hx0", 1)
+        mm_half(1, 0, 0, 0)
+        mm_half(1, 0, 1, 0)
         qx("w1_1", 1)
         tr("w1_2", 1)
-        bias_out()
-        mm(1, 1, 0, 0)
+        th_half(1, 0, 0, 0)
         ev("w1_2", 0, nc.vector.tensor_copy)
-        mm(1, 1, 0, 1)
-        th(1, 1, 0, 0)
-        ev("w1_2", 1, nc.vector.tensor_copy)
+        th_half(1, 0, 1, 0)
+        mm_half(1, 0, 0, 1)
+        mm_half(1, 0, 1, 1)
         mm(1, 1, 0, 2)
+        ev("w1_2", 1, nc.vector.tensor_copy)
+        th_half(1, 0, 0, 1)
         mm(1, 1, 0, 3)
-        th(1, 1, 0, 1)
-        qx("w1_2", 0)
+        th_half(1, 0, 1, 1)
         tr("w1_0", 0)
+        qx("w1_2", 0)
+        th(1, 1, 0, 2)
         qx("w1_2", 1)
         tr("w1_0", 1)
-        th(1, 1, 0, 2)
         ev("w1_0", 0, nc.vector.tensor_copy)
-        mm(1, 2, 0, 0)
         th(1, 1, 0, 3)
+        mm(1, 2, 0, 0)
         mm(1, 2, 0, 1)
         ev("w1_0", 1, nc.vector.tensor_copy)
-        mm(1, 2, 0, 2)
         th(1, 2, 0, 0)
-        qx("w1_0", 0)
+        mm(1, 2, 0, 2)
         mm(1, 2, 0, 3)
-        qx("w1_0", 1)
-        tr("hx1", 0)
+        qx("w1_0", 0)
         th(1, 2, 0, 1)
-        tr("hx1", 1)
-        ev("hx1", 0, nc.vector.tensor_copy)
-        th(1, 2, 0, 2)
+        tr("hx1", 0)
+        qx("w1_0", 1)
         mm(1, 0, 0, 0)
+        th(1, 2, 0, 2)
+        ev("hx1", 0, nc.vector.tensor_copy)
+        tr("hx1", 1)
+        th(1, 2, 0, 3)
         mm(1, 0, 0, 1)
         ev("hx1", 1, nc.vector.tensor_copy)
-        th(1, 2, 0, 3)
-        mm(1, 0, 0, 2)
-        qx("hx1", 0)
         th(1, 0, 0, 0)
+        mm(1, 0, 0, 2)
         mm(1, 0, 0, 3)
-        qx("hx1", 1)
-        tr("w2_1", 0)
-        rg(1, 0)
+        qx("hx1", 0)
         th(1, 0, 0, 1)
-        tr("w2_1", 1)
+        tr("w2_1", 0)
+        qx("hx1", 1)
+        rg(1, 0)
         th(1, 0, 0, 2)
         mm(1, 1, 1, 0)
-        mm(1, 1, 1, 1)
         th(1, 0, 0, 3)
-        ev("w2_1", 0, nc.vector.tensor_copy)
+        mm(1, 1, 1, 1)
         mm(1, 1, 1, 2)
-        qa(1, 0)
+        ev("w2_1", 0, nc.vector.tensor_copy)
         th(1, 1, 1, 0)
+        tr("w2_1", 1)
+        qa(1, 0)
         mm(1, 1, 1, 3)
-        tr("w2_2", 0)
         th(1, 1, 1, 1)
-        ev("w2_1", 1, nc.vector.tensor_copy)
-        tr("w2_2", 1)
-        th(1, 1, 1, 2)
-        qx("w2_1", 0)
         mm(1, 2, 1, 0)
-        qx("w2_1", 1)
+        ev("w2_1", 1, nc.vector.tensor_copy)
+        th(1, 1, 1, 2)
         mm(1, 2, 1, 1)
+        qx("w2_1", 0)
         th(1, 1, 1, 3)
         mm(1, 2, 1, 2)
+        qx("w2_1", 1)
         th(1, 2, 1, 0)
         mm(1, 2, 1, 3)
         rg(1, 1)
-        tr("w2_0", 0)
         th(1, 2, 1, 1)
-        tr("w2_0", 1)
-        th(1, 2, 1, 2)
         mm(1, 0, 1, 0)
-        ev("w2_2", 0, nc.vector.tensor_copy)
+        th(1, 2, 1, 2)
         mm(1, 0, 1, 1)
+        cxh()
         th(1, 2, 1, 3)
-        qa(1, 1)
         mm(1, 0, 1, 2)
         th(1, 0, 1, 0)
+        qa(1, 1)
         mm(1, 0, 1, 3)
-        ev("w2_2", 1, nc.vector.tensor_copy)
         th(1, 0, 1, 1)
         mm(2, 1, 0, 0)
-        qx("w2_2", 0)
-        qx("w2_2", 1)
+        rg(2, 0)
         th(1, 0, 1, 2)
         mm(2, 1, 0, 1)
-        rg(2, 0)
         th(1, 0, 1, 3)
         mm(2, 1, 0, 2)
         th(2, 1, 0, 0)
         mm(2, 1, 0, 3)
-        ev("w2_0", 0, nc.vector.tensor_copy)
+        tr("w2_2", 0)
         th(2, 1, 0, 1)
-        mm(2, 1, 1, 0)
-        qa(2, 0)
+        tr("w2_2", 1)
+        ev("w2_2", 0, nc.vector.tensor_copy)
         th(2, 1, 0, 2)
+        mm(2, 1, 1, 0)
         mm(2, 1, 1, 1)
-        ev("w2_0", 1, nc.vector.tensor_copy)
+        qa(2, 0)
         th(2, 1, 0, 3)
         mm(2, 1, 1, 2)
-        qx("w2_0", 0)
+        ev("w2_2", 1, nc.vector.tensor_copy)
         sg(1, 0, LOW, ALL)
-        qx("w2_0", 1)
         mm(2, 1, 1, 3)
-        rg(0, 0)
+        tr("w2_0", 0)
+        qx("w2_2", 0)
+        qx("w2_2", 1)
+        tr("w2_0", 1)
         sg(1, 0, HIGH, ALL)
-        cxh()
+        rg(0, 0)
         th(2, 1, 1, 0)
+        ev("w2_0", 0, nc.vector.tensor_copy)
         bk(1, 0, 0)
-        qa(0, 0)
-        th(2, 1, 1, 1)
         bk(1, 0, 1)
-        rg(2, 1)
+        th(2, 1, 1, 1)
+        qa(0, 0)
         bk(1, 0, 2)
         th(2, 1, 1, 2)
-        bk(1, 0, 3)
-        mm(2, 2, 0, 0)
+        ev("w2_0", 1, nc.vector.tensor_copy)
         th(2, 1, 1, 3)
-        mm(2, 2, 0, 1)
-        fg(0, 0)
+        qx("w2_0", 0)
+        bk(1, 0, 3)
+        qx("w2_0", 1)
         sg(1, 1, LOW, ALL)
+        mm(2, 2, 0, 0)
+        rg(2, 1)
+        mm(2, 2, 0, 1)
         mm(2, 2, 0, 2)
         mm(2, 2, 0, 3)
-        qa(2, 1)
-        rg(0, 1)
         sg(1, 1, HIGH, ALL)
-        fg(0, 1)
+        fg(0, 0)
+        qa(2, 1)
         th(2, 2, 0, 0)
         bk(1, 1, 0)
-        qa(0, 1)
+        rg(0, 1)
         th(2, 2, 0, 1)
-        bk(1, 1, 1)
-        fg(0, 2)
         th(2, 2, 0, 2)
-        fg(0, 3)
+        fg(0, 1)
         th(2, 2, 0, 3)
-        bk(1, 1, 2)
-        fg(1, 0)
+        qa(0, 1)
+        bk(1, 1, 1)
         sg(2, 0, LOW, ALL)
+        fg(0, 2)
+        fg(0, 3)
+        bk(1, 1, 2)
+        sg(2, 0, HIGH, ALL)
+        fg(1, 0)
         bk(1, 1, 3)
         mm(2, 0, 0, 0)
         fg(1, 1)
+        zc(0, LOW, ALL)
         mm(2, 0, 0, 1)
         fg(1, 2)
-        sg(2, 0, HIGH, ALL)
         mm(2, 0, 0, 2)
         mm(2, 0, 0, 3)
         fg(1, 3)
-        zc(0, LOW, ALL)
         zc(0, HIGH, ALL)
         th(2, 0, 0, 0)
         th(2, 0, 0, 1)
@@ -399,38 +456,47 @@ def tile_lstmcellunknowndata_pa_kernel(tc, hx, cx2, w1, b1, w2, b2, out):
         mm(2, 0, 1, 1)
         th(2, 2, 1, 3)
         mm(2, 0, 1, 2)
-        sg(2, 1, LOW, ALL)
+        th(2, 0, 1, 0)
         mm(2, 0, 1, 3)
         bk(0, 0, 0)
+        th(2, 0, 1, 1)
         bk(0, 0, 1)
         res(0, 0)
-        sg(2, 1, HIGH, ALL)
+        th(2, 0, 1, 2)
         bk(0, 0, 2)
         bk(0, 0, 3)
         res(0, 1)
-        th(2, 0, 1, 0)
-        res(0, 2)
-        th(2, 0, 1, 1)
-        res(0, 3)
-        th(2, 0, 1, 2)
         th(2, 0, 1, 3)
-        zc(1, BOTH, blk(0))
-        sg(0, 1, BOTH, blk(0))
-        zc(1, BOTH, blk(1))
-        pi(1, blk(0))
-        sg(0, 1, BOTH, blk(1))
+        res(0, 2)
+        sg(2, 1, BOTH, blk(0))
         bk(0, 1, 0)
-        zc(1, BOTH, blk(2))
-        pi(1, blk(1))
-        sg(0, 1, BOTH, blk(2))
-        res(1, 0)
         bk(0, 1, 1)
-        zc(1, BOTH, blk(3))
-        pi(1, blk(2))
-        sg(0, 1, BOTH, blk(3))
-        res(1, 1)
+        res(0, 3)
+        sg(2, 1, BOTH, blk(1))
+        zc(1, BOTH, blk(0))
+        sg_back(0, ALL)
+        bk_z(0)
         bk(0, 1, 2)
-        pi(1, blk(3))
-        res(1, 2)
+        sg(2, 1, BOTH, blk(2))
+        pi_back(0, ALL)
+        zc(1, BOTH, blk(1))
+        res_back(0, ALL)
+        sg_back(1, ALL)
+        bk_z(1)
         bk(0, 1, 3)
-        res(1, 3)
+        sg(2, 1, BOTH, blk(3))
+        pi_back(1, ALL)
+        zc(1, BOTH, blk(2))
+        res_back(1, ALL)
+        sg_back(2, ALL)
+        bk_z(2)
+        zc(1, BOTH, blk(3))
+        pi_back(2, ALL)
+        sg_back(3, slice(0, 256))
+        bk_z(3)
+        sg_back(3, slice(256, 512))
+        res_back(2, ALL)
+        pi_back(3, slice(0, 256))
+        pi_back(3, slice(256, 512))
+        res_back(3, slice(0, 256))
+        res_back(3, slice(256, 512))

@@ -89,6 +89,8 @@ def tile_lstmcellunknowndata_pa_kernel(tc, hx, cx2, w1, b1, w2, b2, out):
         warm_out = keep.tile([P, 1], F32, name="warm_out")
         ident = keep.tile([P, P], F32, name="ident")
 
+        warm_mm = keep.tile([P, 512], BF16, name="warm_mm")
+        nc.vector.memset(warm_mm[:], 0.0)
         nc.vector.memset(b1_raw[:], 0.0)
         nc.vector.memset(b2_raw[:], 0.0)
         nc.vector.memset(warm_in[:], 0.0)
@@ -270,21 +272,34 @@ def tile_lstmcellunknowndata_pa_kernel(tc, hx, cx2, w1, b1, w2, b2, out):
                                            in1=live[("f_sb", j)][:, cols], op0=ALU.mult, op1=ALU.add)
             nc.sync.dma_start(out=out_rows[:, j, cols], in_=r_sb[:, cols])
 
+        def warm_up():
+            if "warm_ps" not in live:
+                live["warm_ps"] = psum_mm.tile([P, 512], F32, name="warm_ps", tag="mm")
+            nc.tensor.matmul(out=live["warm_ps"][:], lhsT=warm_mm[:, 0:P], rhs=warm_mm[:], start=True, stop=True)
+
+        warm_up()
+        warm_up()
+        warm_up()
+        warm_up()
+        warm_up()
         tr("w1_1", 0)
         ev("w1_1", 0, nc.scalar.copy)
         tr("hx0", 0)
         bias_cast()
+        warm_up()
         ev("hx0", 0, nc.vector.tensor_copy)
         tr("hx0", 1)
         bias_tr()
         qx("w1_1", 0)
+        warm_up()
         ev("hx0", 1, nc.scalar.copy)
-        tr("w1_1", 1)
         qx("hx0", 0)
+        tr("w1_1", 1)
         bias_out()
+        warm_up()
         ev("w1_1", 1, nc.scalar.copy)
-        tr("w1_2", 0)
         qx("hx0", 1)
+        tr("w1_2", 0)
         mm_half(1, 0, 0, 0)
         mm_half(1, 0, 1, 0)
         qx("w1_1", 1)

@@ -14,13 +14,19 @@ ACT = mybir.ActivationFunctionType
 ALU = mybir.AluOpType
 
 P = 128
+INPUT = 0
+FORGET = 1
+CANDIDATE = 2
 ALL = slice(0, 512)
+LEFT = slice(0, 256)
+RIGHT = slice(256, 512)
 LOW = slice(0, 2)
 HIGH = slice(2, 4)
-BOTH = slice(0, 4)
+FOUR = slice(0, 4)
+IDLE_MATMULS_BEFORE_FIRST_LOAD = 5
 
 
-def blk(jl):
+def block(jl):
     return slice(jl * P, (jl + 1) * P)
 
 
@@ -30,488 +36,329 @@ def tile_lstmcellunknowndata_pa_kernel(tc, hx, cx2, w1, b1, w2, b2, out):
         keep = ctx.enter_context(tc.tile_pool(name="keep", bufs=1))
         stage = ctx.enter_context(tc.tile_pool(name="stage", bufs=4))
         plane_pool = ctx.enter_context(tc.tile_pool(name="plane_pool", bufs=6))
-        t_pool = ctx.enter_context(tc.tile_pool(name="t_pool", bufs=4))
-        f_pool = ctx.enter_context(tc.tile_pool(name="f_pool", bufs=8))
-        outp = ctx.enter_context(tc.tile_pool(name="outp", bufs=4))
-        psum_mm = ctx.enter_context(tc.psum_pool(name="psmm", bufs=4))
-        psum_tp = ctx.enter_context(tc.psum_pool(name="pstp", bufs=8 - 4))
+        forget_pool = ctx.enter_context(tc.tile_pool(name="forget_pool", bufs=8))
+        late_pool = ctx.enter_context(tc.tile_pool(name="late_pool", bufs=4))
+        result_pool = ctx.enter_context(tc.tile_pool(name="result_pool", bufs=4))
+        psum_mx = ctx.enter_context(tc.psum_pool(name="psum_mx", bufs=4))
+        psum_tr = ctx.enter_context(tc.psum_pool(name="psum_tr", bufs=4))
         ctx.enter_context(tc.manual_schedule())
+
         hx_sb = keep.tile([P, 4096], BF16, name="hx_sb")
         cx_sb = keep.tile([P, 4096], BF16, name="cx_sb")
-        hx_c = keep.tile([P, 1024], U32, name="hx_c", align_bytes=64)
-        hx_s = keep.tile([P, 1024], U8, name="hx_s", align_bytes=64)
+        hx_codes = keep.tile([P, 1024], U32, name="hx_codes", align_bytes=64)
+        hx_scales = keep.tile([P, 1024], U8, name="hx_scales", align_bytes=64)
+        hx_rows = hx.rearrange("(p j) k -> p (j k)", j=8)
+        out_rows = out.rearrange("(p j) h -> p j h", j=8)
         raw = {}
         words = {}
         codes = {}
         scales = {}
+        dram = {}
         for c in range(2):
-            raw["hx%d" % c] = hx_sb[:, c * 2048:(c + 1) * 2048]
-            words["hx%d" % c] = hx_sb[:].bitcast(F32)[:, c * 1024:(c + 1) * 1024]
-            codes["hx%d" % c] = hx_c[:, c * 512:(c + 1) * 512]
-            scales["hx%d" % c] = hx_s[:, c * 512:(c + 1) * 512]
+            x = "hx%d" % c
+            raw[x] = hx_sb[:, c * 2048:(c + 1) * 2048]
+            words[x] = hx_sb[:].bitcast(F32)[:, c * 1024:(c + 1) * 1024]
+            codes[x] = hx_codes[:, c * 512:(c + 1) * 512]
+            scales[x] = hx_scales[:, c * 512:(c + 1) * 512]
+            dram[x] = hx_rows[:, c * 2048:(c + 1) * 2048].rearrange("p (s r) -> p s r", s=2)
         for layer in (1, 2):
             for g in range(3):
                 x = "w%d_%d" % (layer, g)
                 w_sb = keep.tile([P, 2048], BF16, name="sb_" + x)
-                w_c = keep.tile([P, 512], U32, name="c_" + x, align_bytes=64)
-                w_s = keep.tile([P, 512], U8, name="s_" + x, align_bytes=64)
+                w_codes = keep.tile([P, 512], U32, name="codes_" + x, align_bytes=64)
+                w_scales = keep.tile([P, 512], U8, name="scales_" + x, align_bytes=64)
                 raw[x] = w_sb[:]
                 words[x] = w_sb[:].bitcast(F32)
-                codes[x] = w_c[:]
-                scales[x] = w_s[:]
-        hx_rows = hx.rearrange("(p j) k -> p (j k)", j=8)
-        dram = {}
-        for c in range(2):
-            dram["hx%d" % c] = hx_rows[:, c * 2048:(c + 1) * 2048].rearrange("p (b x) -> p b x", b=2)
+                codes[x] = w_codes[:]
+                scales[x] = w_scales[:]
         for g in range(3):
             dram["w1_%d" % g] = w1[g].rearrange("(u p e) k -> p u (e k)", u=2, e=2)
-            dram["w2_%d" % g] = w2[g].rearrange("(b t p) f -> p b t f", b=2, p=P)
-
-        def load(x, bk):
-            if bk is None:
-                if x[0:2] == "w2":
-                    nc.sync.dma_start(out=raw[x].rearrange("p (t f) -> p t f", t=4),
-                                      in_=dram[x].rearrange("p b t f -> p (b t) f"))
-                else:
-                    nc.sync.dma_start(out=raw[x].rearrange("p (b x) -> p b x", b=2), in_=dram[x])
-            elif x[0:2] == "w2":
-                nc.sync.dma_start(out=raw[x][:, bk * 1024:(bk + 1) * 1024].rearrange("p (t f) -> p t f", t=2),
-                                  in_=dram[x][:, bk, :, :])
-            else:
-                nc.sync.dma_start(out=raw[x][:, bk * 1024:(bk + 1) * 1024], in_=dram[x][:, bk, :])
+            dram["w2_%d" % g] = w2[g].rearrange("(t p) f -> p t f", p=P)
 
         b1_raw = keep.tile([P, 256], BF16, name="b1_raw")
         b2_raw = keep.tile([P, P], BF16, name="b2_raw")
         b2_f32 = keep.tile([P, P], F32, name="b2_f32")
         b1_words = keep.tile([P, 8], F32, name="b1_words")
         bias = {1: keep.tile([P, 12], F32, name="bias1"), 2: keep.tile([P, 12], F32, name="bias2")}
-        warm_in = keep.tile([P, 1], F32, name="warm_in")
-        warm_out = keep.tile([P, 1], F32, name="warm_out")
+        zeros = keep.tile([P, 512], BF16, name="zeros")
+        table_in = keep.tile([P, 1], F32, name="table_in")
+        table_out = keep.tile([P, 1], F32, name="table_out")
         ident = keep.tile([P, P], F32, name="ident")
+        made = {}
 
-        warm_mm = keep.tile([P, 512], BF16, name="warm_mm")
-        nc.vector.memset(warm_mm[:], 0.0)
-        nc.vector.memset(b1_raw[:], 0.0)
-        nc.vector.memset(b2_raw[:], 0.0)
-        nc.vector.memset(warm_in[:], 0.0)
-        nc.scalar.activation(out=warm_out[:], in_=warm_in[:], func=ACT.Tanh)
-        make_identity(nc, ident[:])
-        load("w1_1", 0)
-        load("hx0", 0)
-        nc.sync.dma_start(out=b1_raw[0:6, :], in_=b1.rearrange("g (u x) -> (g u) x", u=2))
-        nc.sync.dma_start(out=b2_raw[0:12, :], in_=b2.rearrange("g (t x) -> (g t) x", t=4))
-        load("hx0", 1)
-        load("w1_1", 1)
-        load("w1_2", 0)
-        load("w1_2", 1)
-        load("w1_0", 0)
-        load("w1_0", 1)
-        load("hx1", 0)
-        load("hx1", 1)
-        load("w2_1", None)
-        load("w2_2", None)
-        load("w2_0", None)
-        nc.sync.dma_start(out=cx_sb[:], in_=cx2.rearrange("(p j) h -> p (j h)", j=8))
-        live = {}
+        def load(x, half):
+            if x[0:2] == "w2":
+                nc.sync.dma_start(out=raw[x].rearrange("p (t f) -> p t f", t=4), in_=dram[x])
+            elif half is None:
+                nc.sync.dma_start(out=raw[x].rearrange("p (s r) -> p s r", s=2), in_=dram[x])
+            else:
+                nc.sync.dma_start(out=raw[x][:, half * 1024:(half + 1) * 1024], in_=dram[x][:, half, :])
+
+        def idle_matmul():
+            if "idle" not in made:
+                made["idle"] = psum_mx.tile([P, 512], F32, name="idle", tag="mx")
+            nc.tensor.matmul(out=made["idle"][:], lhsT=zeros[:, 0:P], rhs=zeros[:], start=True, stop=True)
+
+        def transpose_in(x, half):
+            bank = psum_tr.tile([P, 2, 256], F32, name="bank_in", tag="tr")
+            made[("bank_in", x, half)] = bank
+            for i in range(2):
+                for u in range(2):
+                    first = (2 * half + i) * 256 + u * P
+                    nc.tensor.transpose(bank[:, u, i * P:(i + 1) * P], words[x][:, first:first + P], ident[:])
+
+        def copy_in(x, half, copy):
+            if ("grouped", x) not in made:
+                made[("grouped", x)] = stage.tile([P, 2048], BF16, name="grouped", tag="grouped", align_bytes=64)
+            grouped_words = made[("grouped", x)][:].bitcast(F32)
+            copy(out=grouped_words[:, half * 512:(half + 1) * 512].rearrange("q (r u) -> q r u", u=2),
+                 in_=made[("bank_in", x, half)][:].rearrange("q u r -> q r u"))
+
+        def quantise_in(x, half):
+            nc.vector.quantize_mx(out=codes[x][:, half * 256:(half + 1) * 256].bitcast(FP8X4),
+                                  scales=scales[x][:, half * 256:(half + 1) * 256],
+                                  in_=made[("grouped", x)][:, half * 1024:(half + 1) * 1024])
+
+        def prepare_on_vector(x):
+            for half in range(2):
+                copy_in(x, half, nc.vector.tensor_copy)
+            for half in range(2):
+                quantise_in(x, half)
 
         def bias_cast():
             nc.gpsimd.tensor_copy(out=b2_f32[:], in_=b2_raw[:])
 
-        def bias_tr():
-            b_ps = psum_tp.tile([P, 2, P], F32, name="b_ps", tag="tp")
-            live["b_ps"] = b_ps
-            nc.tensor.transpose(b_ps[:, 0, :], b1_raw[:].bitcast(F32), ident[:])
-            nc.tensor.transpose(b_ps[:, 1, :], b2_f32[:], ident[:])
+        def bias_transpose():
+            bank = psum_tr.tile([P, 2, P], F32, name="bank_bias", tag="tr")
+            made["bank_bias"] = bank
+            nc.tensor.transpose(bank[:, 0, :], b1_raw[:].bitcast(F32), ident[:])
+            nc.tensor.transpose(bank[:, 1, :], b2_f32[:], ident[:])
 
         def bias_out():
-            b_ps = live["b_ps"]
-            nc.vector.tensor_copy(out=b1_words[:, 0:6], in_=b_ps[:, 0, 0:6])
-            nc.vector.tensor_copy(out=bias[2][:], in_=b_ps[:, 1, 0:12])
+            bank = made["bank_bias"]
+            nc.vector.tensor_copy(out=b1_words[:, 0:6], in_=bank[:, 0, 0:6])
+            nc.vector.tensor_copy(out=bias[2][:], in_=bank[:, 1, 0:12])
             nc.vector.tensor_copy(out=bias[1][:], in_=b1_words[:, 0:6].bitcast(BF16))
 
-        def tr(x, bk):
-            xt = psum_tp.tile([P, 2, 256], F32, name="xt", tag="tp")
-            live[("xt", x, bk)] = xt
-            for i in range(2):
-                for u in range(2):
-                    w0 = (2 * bk + i) * 256 + u * P
-                    nc.tensor.transpose(xt[:, u, i * P:(i + 1) * P], words[x][:, w0:w0 + P], ident[:])
-
-        def ev(x, bk, copy):
-            if ("grouped", x) not in live:
-                live[("grouped", x)] = stage.tile([P, 2048], BF16, name="grouped", tag="grouped", align_bytes=64)
-            g_words = live[("grouped", x)][:].bitcast(F32)
-            copy(out=g_words[:, bk * 512:(bk + 1) * 512].rearrange("q (c u) -> q c u", u=2),
-                 in_=live[("xt", x, bk)][:].rearrange("q u c -> q c u"))
-
-        def qx(x, bk):
-            nc.vector.quantize_mx(out=codes[x][:, bk * 256:(bk + 1) * 256].bitcast(FP8X4),
-                                  scales=scales[x][:, bk * 256:(bk + 1) * 256],
-                                  in_=live[("grouped", x)][:, bk * 1024:(bk + 1) * 1024])
-
-        def mm(layer, g, c, t):
-            ps = psum_mm.tile([P, 512], F32, name="ps", tag="mm")
-            live[("ps", layer, g, c, t)] = ps
+        def multiply(layer, g, c, t, cols):
+            product = psum_mx.tile([P, 512 if cols == ALL else 256], F32, name="product", tag="mx")
+            made[("product", layer, g, c, t, cols == RIGHT)] = product
             x = "w%d_%d" % (layer, g)
             if layer == 1:
-                rhs, rhs_scale = codes["hx%d" % c], scales["hx%d" % c]
+                moving, moving_scales = codes["hx%d" % c], scales["hx%d" % c]
             else:
-                rhs, rhs_scale = live[("a1_c", g, c)][:], live[("a1_s", g, c)][:]
-            nc.tensor.matmul_mx(out=ps[:], lhsT=codes[x][:, t * P:(t + 1) * P].bitcast(FP8X4),
+                moving, moving_scales = made[("hidden_codes", g, c)][:], made[("hidden_scales", g, c)][:]
+            nc.tensor.matmul_mx(out=product[:], lhsT=codes[x][:, t * P:(t + 1) * P].bitcast(FP8X4),
                                 lhsT_scale=scales[x][:, t * P:(t + 1) * P],
-                                rhs=rhs.bitcast(FP8X4), rhs_scale=rhs_scale, start=True, stop=True)
-
-        def mm_half(g, c, t, half):
-            ps = psum_mm.tile([P, 256], F32, name="ps_half", tag="mm")
-            live[("ps_half", g, c, t, half)] = ps
-            x = "w1_%d" % g
-            cols = slice(half * 256, (half + 1) * 256)
-            nc.tensor.matmul_mx(out=ps[:], lhsT=codes[x][:, t * P:(t + 1) * P].bitcast(FP8X4),
-                                lhsT_scale=scales[x][:, t * P:(t + 1) * P],
-                                rhs=codes["hx%d" % c][:, cols].bitcast(FP8X4), rhs_scale=scales["hx%d" % c][:, cols],
+                                rhs=moving[:, cols].bitcast(FP8X4), rhs_scale=moving_scales[:, cols],
                                 start=True, stop=True)
 
-        def th_half(g, c, t, half):
-            if ("planes", g, c) not in live:
-                live[("planes", g, c)] = plane_pool.tile([P, 4, 512], BF16, name="planes", tag="planes")
-            nc.scalar.activation(out=live[("planes", g, c)][:, t, half * 256:(half + 1) * 256],
-                                 in_=live[("ps_half", g, c, t, half)][:], func=ACT.Tanh,
-                                 bias=bias[1][:, g * 4 + t:g * 4 + t + 1], scale=1.0)
+        def activate(layer, g, c, t, cols):
+            key = ("planes", g, c) if layer == 1 else ("gate", g, c)
+            if key not in made:
+                if layer == 1:
+                    made[key] = plane_pool.tile([P, 4, 512], BF16, name="planes", tag="planes")
+                else:
+                    made[key] = keep.tile([P, 4, 512], F32, name="gate%d%d" % (g, c))
+            nc.scalar.activation(out=made[key][:, t, cols], in_=made[("product", layer, g, c, t, cols == RIGHT)][:],
+                                 func=ACT.Tanh, bias=bias[layer][:, 4 * g + t:4 * g + t + 1], scale=1.0)
 
-        def th(layer, g, c, t):
-            if layer == 1:
-                if ("planes", g, c) not in live:
-                    live[("planes", g, c)] = plane_pool.tile([P, 4, 512], BF16, name="planes", tag="planes")
-                dst = live[("planes", g, c)]
-            else:
-                if t == 0:
-                    live[("gate", g, c)] = keep.tile([P, 4, 512], F32, name="gate%d%d" % (g, c))
-                dst = live[("gate", g, c)]
-            nc.scalar.activation(out=dst[:, t, :], in_=live[("ps", layer, g, c, t)][:], func=ACT.Tanh,
-                                 bias=bias[layer][:, g * 4 + t:g * 4 + t + 1], scale=1.0)
+        def layer_on(layer, g, c):
+            for t in range(4):
+                multiply(layer, g, c, t, ALL)
+                activate(layer, g, c, t, ALL)
 
-        def rg(g, c):
-            a1_g = stage.tile([P, 512, 4], BF16, name="a1_g", tag="a1_g", align_bytes=64)
-            live[("a1_g", g, c)] = a1_g
-            nc.vector.tensor_copy(out=a1_g[:].rearrange("p (c i) t -> p c t i", i=4),
-                                  in_=live[("planes", g, c)][:].rearrange("p t (c i) -> p c t i", i=4))
+        def regroup(g, c):
+            grouped = stage.tile([P, 512, 4], BF16, name="hidden_grouped", tag="hidden_grouped", align_bytes=64)
+            made[("hidden_grouped", g, c)] = grouped
+            nc.vector.tensor_copy(out=grouped[:].rearrange("p (r i) t -> p r t i", i=4),
+                                  in_=made[("planes", g, c)][:].rearrange("p t (r i) -> p r t i", i=4))
 
-        def qa(g, c):
-            live[("a1_c", g, c)] = keep.tile([P, 512], U32, name="a1_c%d%d" % (g, c), align_bytes=64)
-            live[("a1_s", g, c)] = keep.tile([P, 512], U8, name="a1_s%d%d" % (g, c), align_bytes=64)
-            nc.vector.quantize_mx(out=live[("a1_c", g, c)][:].bitcast(FP8X4), scales=live[("a1_s", g, c)][:],
-                                  in_=live[("a1_g", g, c)][:].rearrange("p b t -> p (b t)"))
+        def quantise_hidden(g, c):
+            made[("hidden_codes", g, c)] = keep.tile([P, 512], U32, name="hidden_codes%d%d" % (g, c), align_bytes=64)
+            made[("hidden_scales", g, c)] = keep.tile([P, 512], U8, name="hidden_scales%d%d" % (g, c), align_bytes=64)
+            nc.vector.quantize_mx(out=made[("hidden_codes", g, c)][:].bitcast(FP8X4),
+                                  scales=made[("hidden_scales", g, c)][:],
+                                  in_=made[("hidden_grouped", g, c)][:].rearrange("p r t -> p (r t)"))
 
-        def sg(g, c, rows, cols):
-            view = live[("gate", g, c)][:, rows, cols]
+        def hidden_and_operand(g, c, x):
+            regroup(g, c)
+            copy_in(x, 0, nc.vector.tensor_copy)
+            quantise_hidden(g, c)
+            copy_in(x, 1, nc.vector.tensor_copy)
+            quantise_in(x, 0)
+            quantise_in(x, 1)
+
+        def half_tanh(g, c, tiles, cols):
+            view = made[("gate", g, c)][:, tiles, cols]
             nc.scalar.activation(out=view, in_=view, func=ACT.Tanh, scale=0.5)
 
-        def zc(c, rows, cols):
-            view = live[("gate", 2, c)][:, rows, cols]
+        def candidate(c, tiles, cols):
+            view = made[("gate", CANDIDATE, c)][:, tiles, cols]
             nc.scalar.activation(out=view, in_=view, func=ACT.Tanh, bias=0.5, scale=0.5)
 
-        def cxh():
+        def in_two(step, *unit):
+            step(*unit, LOW, ALL)
+            step(*unit, HIGH, ALL)
+
+        def halve_cx():
             nc.vector.tensor_scalar_mul(out=cx_sb[:], in0=cx_sb[:], scalar1=0.5)
 
-        def bk(g, c, jl):
-            ps = psum_tp.tile([P, 512], F32, name="back", tag="tp")
-            live[("back", g, c, jl)] = ps
+        def transpose_out(g, c, jl, pool, tag):
+            bank = pool.tile([P, 512], F32, name="bank_out", tag=tag)
+            made[("bank_out", g, c, jl)] = bank
             for t in range(4):
-                nc.tensor.transpose(ps[:, t * P:(t + 1) * P], live[("gate", g, c)][:, t, blk(jl)], ident[:])
+                nc.tensor.transpose(bank[:, t * P:(t + 1) * P], made[("gate", g, c)][:, t, block(jl)], ident[:])
 
-        def fg(c, jl):
+        def forget_term(c, jl):
             j = 4 * c + jl
-            f_sb = f_pool.tile([P, 512], F32, name="f_sb", tag="f_sb")
-            live[("f_sb", j)] = f_sb
-            nc.vector.scalar_tensor_tensor(out=f_sb[:], in0=live[("back", 1, c, jl)][:], scalar=1.0,
+            term = forget_pool.tile([P, 512], F32, name="forget_term", tag="forget_term")
+            made[("forget_term", j)] = term
+            nc.vector.scalar_tensor_tensor(out=term[:], in0=made[("bank_out", FORGET, c, jl)][:], scalar=1.0,
                                            in1=cx_sb[:, j * 512:(j + 1) * 512], op0=ALU.add, op1=ALU.mult)
 
-        def pi(c, cols):
-            view = live[("gate", 0, c)][:, :, cols]
-            nc.vector.scalar_tensor_tensor(out=view, in0=view, scalar=1.0, in1=live[("gate", 2, c)][:, :, cols],
+        def input_times_candidate(c):
+            view = made[("gate", INPUT, c)][:, :, :]
+            nc.vector.scalar_tensor_tensor(out=view, in0=view, scalar=1.0, in1=made[("gate", CANDIDATE, c)][:, :, :],
                                            op0=ALU.add, op1=ALU.mult)
 
-        out_rows = out.rearrange("(p j) h -> p j h", j=8)
+        def add_and_store(j, product, cols):
+            result = result_pool.tile([P, 512], F32, name="result", tag="result")
+            nc.vector.scalar_tensor_tensor(out=result[:, cols], in0=product, scalar=0.5,
+                                           in1=made[("forget_term", j)][:, cols], op0=ALU.mult, op1=ALU.add)
+            nc.sync.dma_start(out=out_rows[:, j, cols], in_=result[:, cols])
 
-        def res(c, jl):
-            j = 4 * c + jl
-            r_sb = outp.tile([P, 512], F32, name="r_sb", tag="r_sb")
-            nc.vector.scalar_tensor_tensor(out=r_sb[:], in0=live[("back", 0, c, jl)][:], scalar=0.5,
-                                           in1=live[("f_sb", j)][:], op0=ALU.mult, op1=ALU.add)
-            nc.sync.dma_start(out=out_rows[:, j, :], in_=r_sb[:])
-
-        def res_half(c, jl, half):
-            j = 4 * c + jl
-            cols = slice(half * 256, (half + 1) * 256)
-            r_sb = outp.tile([P, 256], F32, name="r_half", tag="r_half")
-            nc.vector.scalar_tensor_tensor(out=r_sb[:], in0=live[("back", 0, c, jl)][:, cols], scalar=0.5,
-                                           in1=live[("f_sb", j)][:, cols], op0=ALU.mult, op1=ALU.add)
-            nc.sync.dma_start(out=out_rows[:, j, cols], in_=r_sb[:])
-
-        def sg_back(jl, cols):
-            if ("t0", jl) not in live:
-                live[("t0", jl)] = t_pool.tile([P, 512], F32, name="t0", tag="t0")
-            nc.scalar.activation(out=live[("t0", jl)][:, cols], in_=live[("back", 0, 1, jl)][:, cols],
+        def late_half_tanh(jl, cols):
+            if ("late", jl) not in made:
+                made[("late", jl)] = late_pool.tile([P, 512], F32, name="late", tag="late")
+            nc.scalar.activation(out=made[("late", jl)][:, cols], in_=made[("bank_out", INPUT, 1, jl)][:, cols],
                                  func=ACT.Tanh, scale=0.5)
 
-        def bk_z(jl):
-            ps = psum_mm.tile([P, 512], F32, name="z_back", tag="mm")
-            live[("z_back", jl)] = ps
-            for t in range(4):
-                nc.tensor.transpose(ps[:, t * P:(t + 1) * P], live[("gate", 2, 1)][:, t, blk(jl)], ident[:])
-
-        def pi_back(jl, cols):
-            view = live[("t0", jl)][:, cols]
-            nc.vector.scalar_tensor_tensor(out=view, in0=view, scalar=1.0, in1=live[("z_back", jl)][:, cols],
+        def late_times_candidate(jl, cols):
+            view = made[("late", jl)][:, cols]
+            nc.vector.scalar_tensor_tensor(out=view, in0=view, scalar=1.0,
+                                           in1=made[("bank_out", CANDIDATE, 1, jl)][:, cols],
                                            op0=ALU.add, op1=ALU.mult)
 
-        def res_back(jl, cols):
-            j = 4 + jl
-            r_sb = outp.tile([P, 512], F32, name="r_back", tag="r_sb")
-            nc.vector.scalar_tensor_tensor(out=r_sb[:, cols], in0=live[("t0", jl)][:, cols], scalar=0.5,
-                                           in1=live[("f_sb", j)][:, cols], op0=ALU.mult, op1=ALU.add)
-            nc.sync.dma_start(out=out_rows[:, j, cols], in_=r_sb[:, cols])
+        nc.vector.memset(zeros[:], 0.0)
+        nc.vector.memset(b1_raw[:], 0.0)
+        nc.vector.memset(b2_raw[:], 0.0)
+        nc.vector.memset(table_in[:], 0.0)
+        nc.scalar.activation(out=table_out[:], in_=table_in[:], func=ACT.Tanh)
+        make_identity(nc, ident[:])
 
-        def warm_up():
-            if "warm_ps" not in live:
-                live["warm_ps"] = psum_mm.tile([P, 512], F32, name="warm_ps", tag="mm")
-            nc.tensor.matmul(out=live["warm_ps"][:], lhsT=warm_mm[:, 0:P], rhs=warm_mm[:], start=True, stop=True)
+        load("w1_1", 0)
+        load("hx0", 0)
+        nc.sync.dma_start(out=b1_raw[0:6, :], in_=b1.rearrange("g (u r) -> (g u) r", u=2))
+        nc.sync.dma_start(out=b2_raw[0:12, :], in_=b2.rearrange("g (t r) -> (g t) r", t=4))
+        load("hx0", 1)
+        load("w1_1", 1)
+        for x in ("w1_2", "w1_0", "hx1"):
+            load(x, 0)
+            load(x, 1)
+        for x in ("w2_1", "w2_2", "w2_0"):
+            load(x, None)
+        nc.sync.dma_start(out=cx_sb[:], in_=cx2.rearrange("(p j) h -> p (j h)", j=8))
 
-        warm_up()
-        warm_up()
-        warm_up()
-        warm_up()
-        warm_up()
-        tr("w1_1", 0)
-        ev("w1_1", 0, nc.scalar.copy)
-        tr("hx0", 0)
+        for i in range(IDLE_MATMULS_BEFORE_FIRST_LOAD):
+            idle_matmul()
+        transpose_in("w1_1", 0)
+        copy_in("w1_1", 0, nc.scalar.copy)
+        transpose_in("hx0", 0)
+        idle_matmul()
+        copy_in("hx0", 0, nc.vector.tensor_copy)
+        transpose_in("hx0", 1)
+        copy_in("hx0", 1, nc.scalar.copy)
         bias_cast()
-        warm_up()
-        ev("hx0", 0, nc.vector.tensor_copy)
-        tr("hx0", 1)
-        bias_tr()
-        qx("w1_1", 0)
-        warm_up()
-        ev("hx0", 1, nc.scalar.copy)
-        qx("hx0", 0)
-        tr("w1_1", 1)
+        bias_transpose()
+        idle_matmul()
+        quantise_in("w1_1", 0)
+        quantise_in("hx0", 0)
         bias_out()
-        warm_up()
-        ev("w1_1", 1, nc.scalar.copy)
-        qx("hx0", 1)
-        tr("w1_2", 0)
-        mm_half(1, 0, 0, 0)
-        mm_half(1, 0, 1, 0)
-        qx("w1_1", 1)
-        tr("w1_2", 1)
-        th_half(1, 0, 0, 0)
-        ev("w1_2", 0, nc.vector.tensor_copy)
-        th_half(1, 0, 1, 0)
-        mm_half(1, 0, 0, 1)
-        mm_half(1, 0, 1, 1)
-        mm(1, 1, 0, 2)
-        ev("w1_2", 1, nc.vector.tensor_copy)
-        th_half(1, 0, 0, 1)
-        mm(1, 1, 0, 3)
-        th_half(1, 0, 1, 1)
-        tr("w1_0", 0)
-        qx("w1_2", 0)
-        th(1, 1, 0, 2)
-        qx("w1_2", 1)
-        tr("w1_0", 1)
-        ev("w1_0", 0, nc.vector.tensor_copy)
-        th(1, 1, 0, 3)
-        mm(1, 2, 0, 0)
-        mm(1, 2, 0, 1)
-        ev("w1_0", 1, nc.vector.tensor_copy)
-        th(1, 2, 0, 0)
-        mm(1, 2, 0, 2)
-        mm(1, 2, 0, 3)
-        qx("w1_0", 0)
-        th(1, 2, 0, 1)
-        tr("hx1", 0)
-        qx("w1_0", 1)
-        mm(1, 0, 0, 0)
-        th(1, 2, 0, 2)
-        ev("hx1", 0, nc.vector.tensor_copy)
-        tr("hx1", 1)
-        th(1, 2, 0, 3)
-        mm(1, 0, 0, 1)
-        ev("hx1", 1, nc.vector.tensor_copy)
-        th(1, 0, 0, 0)
-        mm(1, 0, 0, 2)
-        mm(1, 0, 0, 3)
-        qx("hx1", 0)
-        th(1, 0, 0, 1)
-        tr("w2_1", 0)
-        qx("hx1", 1)
-        rg(1, 0)
-        th(1, 0, 0, 2)
-        mm(1, 1, 1, 0)
-        th(1, 0, 0, 3)
-        mm(1, 1, 1, 1)
-        mm(1, 1, 1, 2)
-        ev("w2_1", 0, nc.vector.tensor_copy)
-        th(1, 1, 1, 0)
-        tr("w2_1", 1)
-        qa(1, 0)
-        mm(1, 1, 1, 3)
-        th(1, 1, 1, 1)
-        mm(1, 2, 1, 0)
-        ev("w2_1", 1, nc.vector.tensor_copy)
-        th(1, 1, 1, 2)
-        mm(1, 2, 1, 1)
-        qx("w2_1", 0)
-        th(1, 1, 1, 3)
-        mm(1, 2, 1, 2)
-        qx("w2_1", 1)
-        th(1, 2, 1, 0)
-        mm(1, 2, 1, 3)
-        rg(1, 1)
-        th(1, 2, 1, 1)
-        mm(1, 0, 1, 0)
-        th(1, 2, 1, 2)
-        mm(1, 0, 1, 1)
-        cxh()
-        th(1, 2, 1, 3)
-        mm(1, 0, 1, 2)
-        th(1, 0, 1, 0)
-        qa(1, 1)
-        mm(1, 0, 1, 3)
-        th(1, 0, 1, 1)
-        mm(2, 1, 0, 0)
-        rg(2, 0)
-        th(1, 0, 1, 2)
-        mm(2, 1, 0, 1)
-        th(1, 0, 1, 3)
-        mm(2, 1, 0, 2)
-        th(2, 1, 0, 0)
-        mm(2, 1, 0, 3)
-        tr("w2_2", 0)
-        th(2, 1, 0, 1)
-        tr("w2_2", 1)
-        ev("w2_2", 0, nc.vector.tensor_copy)
-        th(2, 1, 0, 2)
-        mm(2, 1, 1, 0)
-        mm(2, 1, 1, 1)
-        qa(2, 0)
-        th(2, 1, 0, 3)
-        mm(2, 1, 1, 2)
-        ev("w2_2", 1, nc.vector.tensor_copy)
-        sg(1, 0, LOW, ALL)
-        mm(2, 1, 1, 3)
-        tr("w2_0", 0)
-        qx("w2_2", 0)
-        qx("w2_2", 1)
-        tr("w2_0", 1)
-        sg(1, 0, HIGH, ALL)
-        rg(0, 0)
-        th(2, 1, 1, 0)
-        ev("w2_0", 0, nc.vector.tensor_copy)
-        bk(1, 0, 0)
-        bk(1, 0, 1)
-        th(2, 1, 1, 1)
-        qa(0, 0)
-        bk(1, 0, 2)
-        th(2, 1, 1, 2)
-        ev("w2_0", 1, nc.vector.tensor_copy)
-        th(2, 1, 1, 3)
-        qx("w2_0", 0)
-        bk(1, 0, 3)
-        qx("w2_0", 1)
-        sg(1, 1, LOW, ALL)
-        mm(2, 2, 0, 0)
-        rg(2, 1)
-        mm(2, 2, 0, 1)
-        mm(2, 2, 0, 2)
-        mm(2, 2, 0, 3)
-        sg(1, 1, HIGH, ALL)
-        fg(0, 0)
-        qa(2, 1)
-        th(2, 2, 0, 0)
-        bk(1, 1, 0)
-        rg(0, 1)
-        th(2, 2, 0, 1)
-        th(2, 2, 0, 2)
-        fg(0, 1)
-        th(2, 2, 0, 3)
-        qa(0, 1)
-        bk(1, 1, 1)
-        sg(2, 0, LOW, ALL)
-        fg(0, 2)
-        fg(0, 3)
-        bk(1, 1, 2)
-        sg(2, 0, HIGH, ALL)
-        fg(1, 0)
-        bk(1, 1, 3)
-        mm(2, 0, 0, 0)
-        fg(1, 1)
-        zc(0, LOW, ALL)
-        mm(2, 0, 0, 1)
-        fg(1, 2)
-        mm(2, 0, 0, 2)
-        mm(2, 0, 0, 3)
-        fg(1, 3)
-        zc(0, HIGH, ALL)
-        th(2, 0, 0, 0)
-        th(2, 0, 0, 1)
-        mm(2, 2, 1, 0)
-        th(2, 0, 0, 2)
-        mm(2, 2, 1, 1)
-        th(2, 0, 0, 3)
-        mm(2, 2, 1, 2)
-        sg(0, 0, LOW, ALL)
-        mm(2, 2, 1, 3)
-        sg(0, 0, HIGH, ALL)
-        th(2, 2, 1, 0)
-        pi(0, ALL)
-        th(2, 2, 1, 1)
-        mm(2, 0, 1, 0)
-        th(2, 2, 1, 2)
-        mm(2, 0, 1, 1)
-        th(2, 2, 1, 3)
-        mm(2, 0, 1, 2)
-        th(2, 0, 1, 0)
-        mm(2, 0, 1, 3)
-        bk(0, 0, 0)
-        th(2, 0, 1, 1)
-        bk(0, 0, 1)
-        res(0, 0)
-        th(2, 0, 1, 2)
-        bk(0, 0, 2)
-        bk(0, 0, 3)
-        res(0, 1)
-        th(2, 0, 1, 3)
-        res(0, 2)
-        sg(2, 1, BOTH, blk(0))
-        bk(0, 1, 0)
-        bk(0, 1, 1)
-        res(0, 3)
-        sg(2, 1, BOTH, blk(1))
-        zc(1, BOTH, blk(0))
-        sg_back(0, ALL)
-        bk_z(0)
-        bk(0, 1, 2)
-        sg(2, 1, BOTH, blk(2))
-        pi_back(0, ALL)
-        zc(1, BOTH, blk(1))
-        res_back(0, ALL)
-        sg_back(1, ALL)
-        bk_z(1)
-        bk(0, 1, 3)
-        sg(2, 1, BOTH, blk(3))
-        pi_back(1, ALL)
-        zc(1, BOTH, blk(2))
-        res_back(1, ALL)
-        sg_back(2, ALL)
-        bk_z(2)
-        zc(1, BOTH, blk(3))
-        pi_back(2, ALL)
-        sg_back(3, slice(0, 256))
-        bk_z(3)
-        sg_back(3, slice(256, 512))
-        res_back(2, ALL)
-        pi_back(3, slice(0, 256))
-        pi_back(3, slice(256, 512))
-        res_back(3, slice(0, 256))
-        res_back(3, slice(256, 512))
+        transpose_in("w1_1", 1)
+        idle_matmul()
+        copy_in("w1_1", 1, nc.scalar.copy)
+        quantise_in("hx0", 1)
+        quantise_in("w1_1", 1)
+        transpose_in("w1_2", 0)
+
+        for cols in (LEFT, RIGHT):
+            for t in range(2):
+                multiply(1, FORGET, 0, t, cols)
+            if cols == LEFT:
+                transpose_in("w1_2", 1)
+            for t in range(2):
+                activate(1, FORGET, 0, t, cols)
+        for t in range(2, 4):
+            multiply(1, FORGET, 0, t, ALL)
+            activate(1, FORGET, 0, t, ALL)
+        prepare_on_vector("w1_2")
+        for half in range(2):
+            transpose_in("w1_0", half)
+        prepare_on_vector("w1_0")
+        layer_on(1, CANDIDATE, 0)
+        for half in range(2):
+            transpose_in("hx1", half)
+        prepare_on_vector("hx1")
+        layer_on(1, INPUT, 0)
+        for half in range(2):
+            transpose_in("w2_1", half)
+        hidden_and_operand(FORGET, 0, "w2_1")
+        layer_on(1, FORGET, 1)
+        regroup(FORGET, 1)
+        halve_cx()
+        quantise_hidden(FORGET, 1)
+        layer_on(1, CANDIDATE, 1)
+        layer_on(1, INPUT, 1)
+
+        layer_on(2, FORGET, 0)
+        in_two(half_tanh, FORGET, 0)
+        for half in range(2):
+            transpose_in("w2_2", half)
+        hidden_and_operand(CANDIDATE, 0, "w2_2")
+        layer_on(2, FORGET, 1)
+        in_two(half_tanh, FORGET, 1)
+        for half in range(2):
+            transpose_in("w2_0", half)
+        hidden_and_operand(INPUT, 0, "w2_0")
+        for jl in range(4):
+            transpose_out(FORGET, 0, jl, psum_tr, "tr")
+        regroup(CANDIDATE, 1)
+        forget_term(0, 0)
+        quantise_hidden(CANDIDATE, 1)
+        regroup(INPUT, 1)
+        forget_term(0, 1)
+        quantise_hidden(INPUT, 1)
+        forget_term(0, 2)
+        forget_term(0, 3)
+        layer_on(2, CANDIDATE, 0)
+        in_two(half_tanh, CANDIDATE, 0)
+        in_two(candidate, 0)
+        for jl in range(4):
+            transpose_out(FORGET, 1, jl, psum_tr, "tr")
+            forget_term(1, jl)
+        layer_on(2, INPUT, 0)
+        in_two(half_tanh, INPUT, 0)
+        input_times_candidate(0)
+        layer_on(2, CANDIDATE, 1)
+        layer_on(2, INPUT, 1)
+        for jl in range(4):
+            transpose_out(INPUT, 0, jl, psum_tr, "tr")
+            add_and_store(jl, made[("bank_out", INPUT, 0, jl)][:], ALL)
+
+        for jl in range(2):
+            transpose_out(INPUT, 1, jl, psum_tr, "tr")
+            half_tanh(CANDIDATE, 1, FOUR, block(jl))
+        for jl in range(4):
+            pieces = (ALL,) if jl < 3 else (LEFT, RIGHT)
+            candidate(1, FOUR, block(jl))
+            transpose_out(CANDIDATE, 1, jl, psum_mx, "mx")
+            for cols in pieces:
+                late_half_tanh(jl, cols)
+            if jl < 2:
+                transpose_out(INPUT, 1, jl + 2, psum_tr, "tr")
+                half_tanh(CANDIDATE, 1, FOUR, block(jl + 2))
+            for cols in pieces:
+                late_times_candidate(jl, cols)
+            for cols in pieces:
+                add_and_store(4 + jl, made[("late", jl)][:, cols], cols)

@@ -26,7 +26,7 @@ FOUR = slice(0, 4)
 IDLE_MATMULS_BEFORE_FIRST_LOAD = 5
 
 
-def block(jl):
+def strip(jl):
     return slice(jl * P, (jl + 1) * P)
 
 
@@ -50,14 +50,14 @@ def tile_lstmcellunknowndata_pa_kernel(tc, hx, cx2, w1, b1, w2, b2, out):
         hx_rows = hx.rearrange("(p j) k -> p (j k)", j=8)
         out_rows = out.rearrange("(p j) h -> p j h", j=8)
         raw = {}
-        words = {}
+        pairs = {}
         codes = {}
         scales = {}
         dram = {}
         for c in range(2):
             x = "hx%d" % c
             raw[x] = hx_sb[:, c * 2048:(c + 1) * 2048]
-            words[x] = hx_sb[:].bitcast(F32)[:, c * 1024:(c + 1) * 1024]
+            pairs[x] = hx_sb[:].bitcast(F32)[:, c * 1024:(c + 1) * 1024]
             codes[x] = hx_codes[:, c * 512:(c + 1) * 512]
             scales[x] = hx_scales[:, c * 512:(c + 1) * 512]
             dram[x] = hx_rows[:, c * 2048:(c + 1) * 2048].rearrange("p (s r) -> p s r", s=2)
@@ -68,7 +68,7 @@ def tile_lstmcellunknowndata_pa_kernel(tc, hx, cx2, w1, b1, w2, b2, out):
                 w_codes = keep.tile([P, 512], U32, name="codes_" + x, align_bytes=64)
                 w_scales = keep.tile([P, 512], U8, name="scales_" + x, align_bytes=64)
                 raw[x] = w_sb[:]
-                words[x] = w_sb[:].bitcast(F32)
+                pairs[x] = w_sb[:].bitcast(F32)
                 codes[x] = w_codes[:]
                 scales[x] = w_scales[:]
         for g in range(3):
@@ -78,7 +78,7 @@ def tile_lstmcellunknowndata_pa_kernel(tc, hx, cx2, w1, b1, w2, b2, out):
         b1_raw = keep.tile([P, 256], BF16, name="b1_raw")
         b2_raw = keep.tile([P, P], BF16, name="b2_raw")
         b2_f32 = keep.tile([P, P], F32, name="b2_f32")
-        b1_words = keep.tile([P, 8], F32, name="b1_words")
+        b1_pairs = keep.tile([P, 8], F32, name="b1_pairs")
         bias = {1: keep.tile([P, 12], F32, name="bias1"), 2: keep.tile([P, 12], F32, name="bias2")}
         zeros = keep.tile([P, 512], BF16, name="zeros")
         table_in = keep.tile([P, 1], F32, name="table_in")
@@ -86,44 +86,47 @@ def tile_lstmcellunknowndata_pa_kernel(tc, hx, cx2, w1, b1, w2, b2, out):
         ident = keep.tile([P, P], F32, name="ident")
         made = {}
 
-        def load(x, half):
-            if x[0:2] == "w2":
-                nc.sync.dma_start(out=raw[x].rearrange("p (t f) -> p t f", t=4), in_=dram[x])
-            elif half is None:
-                nc.sync.dma_start(out=raw[x].rearrange("p (s r) -> p s r", s=2), in_=dram[x])
-            else:
-                nc.sync.dma_start(out=raw[x][:, half * 1024:(half + 1) * 1024], in_=dram[x][:, half, :])
+        def load_part(x, part):
+            nc.sync.dma_start(out=raw[x][:, part * 1024:(part + 1) * 1024], in_=dram[x][:, part, :])
+
+        def load_w2(g):
+            x = "w2_%d" % g
+            nc.sync.dma_start(out=raw[x].rearrange("p (t f) -> p t f", t=4), in_=dram[x])
 
         def idle_matmul():
             if "idle" not in made:
                 made["idle"] = psum_mx.tile([P, 512], F32, name="idle", tag="mx")
             nc.tensor.matmul(out=made["idle"][:], lhsT=zeros[:, 0:P], rhs=zeros[:], start=True, stop=True)
 
-        def transpose_in(x, half):
+        def transpose_in(x, part):
             bank = psum_tr.tile([P, 2, 256], F32, name="bank_in", tag="tr")
-            made[("bank_in", x, half)] = bank
+            made[("bank_in", x, part)] = bank
             for i in range(2):
                 for u in range(2):
-                    first = (2 * half + i) * 256 + u * P
-                    nc.tensor.transpose(bank[:, u, i * P:(i + 1) * P], words[x][:, first:first + P], ident[:])
+                    first = (2 * part + i) * 256 + u * P
+                    nc.tensor.transpose(bank[:, u, i * P:(i + 1) * P], pairs[x][:, first:first + P], ident[:])
 
-        def copy_in(x, half, copy):
+        def copy_in(x, part, copy):
             if ("grouped", x) not in made:
                 made[("grouped", x)] = stage.tile([P, 2048], BF16, name="grouped", tag="grouped", align_bytes=64)
-            grouped_words = made[("grouped", x)][:].bitcast(F32)
-            copy(out=grouped_words[:, half * 512:(half + 1) * 512].rearrange("q (r u) -> q r u", u=2),
-                 in_=made[("bank_in", x, half)][:].rearrange("q u r -> q r u"))
+            grouped_pairs = made[("grouped", x)][:].bitcast(F32)
+            copy(out=grouped_pairs[:, part * 512:(part + 1) * 512].rearrange("q (r u) -> q r u", u=2),
+                 in_=made[("bank_in", x, part)][:].rearrange("q u r -> q r u"))
 
-        def quantise_in(x, half):
-            nc.vector.quantize_mx(out=codes[x][:, half * 256:(half + 1) * 256].bitcast(FP8X4),
-                                  scales=scales[x][:, half * 256:(half + 1) * 256],
-                                  in_=made[("grouped", x)][:, half * 1024:(half + 1) * 1024])
+        def quantise_in(x, part):
+            nc.vector.quantize_mx(out=codes[x][:, part * 256:(part + 1) * 256].bitcast(FP8X4),
+                                  scales=scales[x][:, part * 256:(part + 1) * 256],
+                                  in_=made[("grouped", x)][:, part * 1024:(part + 1) * 1024])
+
+        def transpose_operand(x):
+            for part in range(2):
+                transpose_in(x, part)
 
         def prepare_on_vector(x):
-            for half in range(2):
-                copy_in(x, half, nc.vector.tensor_copy)
-            for half in range(2):
-                quantise_in(x, half)
+            for part in range(2):
+                copy_in(x, part, nc.vector.tensor_copy)
+            for part in range(2):
+                quantise_in(x, part)
 
         def bias_cast():
             nc.gpsimd.tensor_copy(out=b2_f32[:], in_=b2_raw[:])
@@ -136,9 +139,9 @@ def tile_lstmcellunknowndata_pa_kernel(tc, hx, cx2, w1, b1, w2, b2, out):
 
         def bias_out():
             bank = made["bank_bias"]
-            nc.vector.tensor_copy(out=b1_words[:, 0:6], in_=bank[:, 0, 0:6])
+            nc.vector.tensor_copy(out=b1_pairs[:, 0:6], in_=bank[:, 0, 0:6])
             nc.vector.tensor_copy(out=bias[2][:], in_=bank[:, 1, 0:12])
-            nc.vector.tensor_copy(out=bias[1][:], in_=b1_words[:, 0:6].bitcast(BF16))
+            nc.vector.tensor_copy(out=bias[1][:], in_=b1_pairs[:, 0:6].bitcast(BF16))
 
         def multiply(layer, g, c, t, cols):
             product = psum_mx.tile([P, 512 if cols == ALL else 256], F32, name="product", tag="mx")
@@ -189,17 +192,17 @@ def tile_lstmcellunknowndata_pa_kernel(tc, hx, cx2, w1, b1, w2, b2, out):
             quantise_in(x, 0)
             quantise_in(x, 1)
 
-        def half_tanh(g, c, tiles, cols):
+        def sigmoid_stage(g, c, tiles, cols):
             view = made[("gate", g, c)][:, tiles, cols]
             nc.scalar.activation(out=view, in_=view, func=ACT.Tanh, scale=0.5)
 
-        def candidate(c, tiles, cols):
+        def candidate_stage(c, tiles, cols):
             view = made[("gate", CANDIDATE, c)][:, tiles, cols]
             nc.scalar.activation(out=view, in_=view, func=ACT.Tanh, bias=0.5, scale=0.5)
 
-        def in_two(step, *unit):
-            step(*unit, LOW, ALL)
-            step(*unit, HIGH, ALL)
+        def in_two(stage_step, *unit):
+            stage_step(*unit, LOW, ALL)
+            stage_step(*unit, HIGH, ALL)
 
         def halve_cx():
             nc.vector.tensor_scalar_mul(out=cx_sb[:], in0=cx_sb[:], scalar1=0.5)
@@ -208,7 +211,7 @@ def tile_lstmcellunknowndata_pa_kernel(tc, hx, cx2, w1, b1, w2, b2, out):
             bank = pool.tile([P, 512], F32, name="bank_out", tag=tag)
             made[("bank_out", g, c, jl)] = bank
             for t in range(4):
-                nc.tensor.transpose(bank[:, t * P:(t + 1) * P], made[("gate", g, c)][:, t, block(jl)], ident[:])
+                nc.tensor.transpose(bank[:, t * P:(t + 1) * P], made[("gate", g, c)][:, t, strip(jl)], ident[:])
 
         def forget_term(c, jl):
             j = 4 * c + jl
@@ -222,13 +225,13 @@ def tile_lstmcellunknowndata_pa_kernel(tc, hx, cx2, w1, b1, w2, b2, out):
             nc.vector.scalar_tensor_tensor(out=view, in0=view, scalar=1.0, in1=made[("gate", CANDIDATE, c)][:, :, :],
                                            op0=ALU.add, op1=ALU.mult)
 
-        def add_and_store(j, product, cols):
+        def add_and_store(j, gated, cols):
             result = result_pool.tile([P, 512], F32, name="result", tag="result")
-            nc.vector.scalar_tensor_tensor(out=result[:, cols], in0=product, scalar=0.5,
+            nc.vector.scalar_tensor_tensor(out=result[:, cols], in0=gated, scalar=0.5,
                                            in1=made[("forget_term", j)][:, cols], op0=ALU.mult, op1=ALU.add)
             nc.sync.dma_start(out=out_rows[:, j, cols], in_=result[:, cols])
 
-        def late_half_tanh(jl, cols):
+        def late_sigmoid_stage(jl, cols):
             if ("late", jl) not in made:
                 made[("late", jl)] = late_pool.tile([P, 512], F32, name="late", tag="late")
             nc.scalar.activation(out=made[("late", jl)][:, cols], in_=made[("bank_out", INPUT, 1, jl)][:, cols],
@@ -247,17 +250,17 @@ def tile_lstmcellunknowndata_pa_kernel(tc, hx, cx2, w1, b1, w2, b2, out):
         nc.scalar.activation(out=table_out[:], in_=table_in[:], func=ACT.Tanh)
         make_identity(nc, ident[:])
 
-        load("w1_1", 0)
-        load("hx0", 0)
+        load_part("w1_1", 0)
+        load_part("hx0", 0)
         nc.sync.dma_start(out=b1_raw[0:6, :], in_=b1.rearrange("g (u r) -> (g u) r", u=2))
         nc.sync.dma_start(out=b2_raw[0:12, :], in_=b2.rearrange("g (t r) -> (g t) r", t=4))
-        load("hx0", 1)
-        load("w1_1", 1)
+        load_part("hx0", 1)
+        load_part("w1_1", 1)
         for x in ("w1_2", "w1_0", "hx1"):
-            load(x, 0)
-            load(x, 1)
-        for x in ("w2_1", "w2_2", "w2_0"):
-            load(x, None)
+            load_part(x, 0)
+            load_part(x, 1)
+        for g in (FORGET, CANDIDATE, INPUT):
+            load_w2(g)
         nc.sync.dma_start(out=cx_sb[:], in_=cx2.rearrange("(p j) h -> p (j h)", j=8))
 
         for i in range(IDLE_MATMULS_BEFORE_FIRST_LOAD):
@@ -293,16 +296,13 @@ def tile_lstmcellunknowndata_pa_kernel(tc, hx, cx2, w1, b1, w2, b2, out):
             multiply(1, FORGET, 0, t, ALL)
             activate(1, FORGET, 0, t, ALL)
         prepare_on_vector("w1_2")
-        for half in range(2):
-            transpose_in("w1_0", half)
+        transpose_operand("w1_0")
         prepare_on_vector("w1_0")
         layer_on(1, CANDIDATE, 0)
-        for half in range(2):
-            transpose_in("hx1", half)
+        transpose_operand("hx1")
         prepare_on_vector("hx1")
         layer_on(1, INPUT, 0)
-        for half in range(2):
-            transpose_in("w2_1", half)
+        transpose_operand("w2_1")
         hidden_and_operand(FORGET, 0, "w2_1")
         layer_on(1, FORGET, 1)
         regroup(FORGET, 1)
@@ -312,14 +312,12 @@ def tile_lstmcellunknowndata_pa_kernel(tc, hx, cx2, w1, b1, w2, b2, out):
         layer_on(1, INPUT, 1)
 
         layer_on(2, FORGET, 0)
-        in_two(half_tanh, FORGET, 0)
-        for half in range(2):
-            transpose_in("w2_2", half)
+        in_two(sigmoid_stage, FORGET, 0)
+        transpose_operand("w2_2")
         hidden_and_operand(CANDIDATE, 0, "w2_2")
         layer_on(2, FORGET, 1)
-        in_two(half_tanh, FORGET, 1)
-        for half in range(2):
-            transpose_in("w2_0", half)
+        in_two(sigmoid_stage, FORGET, 1)
+        transpose_operand("w2_0")
         hidden_and_operand(INPUT, 0, "w2_0")
         for jl in range(4):
             transpose_out(FORGET, 0, jl, psum_tr, "tr")
@@ -332,13 +330,13 @@ def tile_lstmcellunknowndata_pa_kernel(tc, hx, cx2, w1, b1, w2, b2, out):
         forget_term(0, 2)
         forget_term(0, 3)
         layer_on(2, CANDIDATE, 0)
-        in_two(half_tanh, CANDIDATE, 0)
-        in_two(candidate, 0)
+        in_two(sigmoid_stage, CANDIDATE, 0)
+        in_two(candidate_stage, 0)
         for jl in range(4):
             transpose_out(FORGET, 1, jl, psum_tr, "tr")
             forget_term(1, jl)
         layer_on(2, INPUT, 0)
-        in_two(half_tanh, INPUT, 0)
+        in_two(sigmoid_stage, INPUT, 0)
         input_times_candidate(0)
         layer_on(2, CANDIDATE, 1)
         layer_on(2, INPUT, 1)
@@ -348,16 +346,16 @@ def tile_lstmcellunknowndata_pa_kernel(tc, hx, cx2, w1, b1, w2, b2, out):
 
         for jl in range(2):
             transpose_out(INPUT, 1, jl, psum_tr, "tr")
-            half_tanh(CANDIDATE, 1, FOUR, block(jl))
+            sigmoid_stage(CANDIDATE, 1, FOUR, strip(jl))
         for jl in range(4):
             pieces = (ALL,) if jl < 3 else (LEFT, RIGHT)
-            candidate(1, FOUR, block(jl))
+            candidate_stage(1, FOUR, strip(jl))
             transpose_out(CANDIDATE, 1, jl, psum_mx, "mx")
             for cols in pieces:
-                late_half_tanh(jl, cols)
+                late_sigmoid_stage(jl, cols)
             if jl < 2:
                 transpose_out(INPUT, 1, jl + 2, psum_tr, "tr")
-                half_tanh(CANDIDATE, 1, FOUR, block(jl + 2))
+                sigmoid_stage(CANDIDATE, 1, FOUR, strip(jl + 2))
             for cols in pieces:
                 late_times_candidate(jl, cols)
             for cols in pieces:

@@ -34,7 +34,7 @@ def tile_lstmcellunknowndata_pa_kernel(tc, hx, cx2, w1, b1, w2, b2, out):
     nc = tc.nc
     with ExitStack() as ctx:
         keep = ctx.enter_context(tc.tile_pool(name="keep", bufs=1))
-        stage = ctx.enter_context(tc.tile_pool(name="stage", bufs=4))
+        staging = ctx.enter_context(tc.tile_pool(name="stage", bufs=4))
         plane_pool = ctx.enter_context(tc.tile_pool(name="plane_pool", bufs=6))
         forget_pool = ctx.enter_context(tc.tile_pool(name="forget_pool", bufs=8))
         late_pool = ctx.enter_context(tc.tile_pool(name="late_pool", bufs=4))
@@ -93,10 +93,10 @@ def tile_lstmcellunknowndata_pa_kernel(tc, hx, cx2, w1, b1, w2, b2, out):
             x = "w2_%d" % g
             nc.sync.dma_start(out=raw[x].rearrange("p (t f) -> p t f", t=4), in_=dram[x])
 
-        def idle_matmul():
-            if "idle" not in made:
-                made["idle"] = psum_mx.tile([P, 512], F32, name="idle", tag="mx")
-            nc.tensor.matmul(out=made["idle"][:], lhsT=zeros[:, 0:P], rhs=zeros[:], start=True, stop=True)
+        def idle_matmul(phase):
+            if ("idle", phase) not in made:
+                made[("idle", phase)] = psum_mx.tile([P, 512], F32, name="idle", tag="mx")
+            nc.tensor.matmul(out=made[("idle", phase)][:], lhsT=zeros[:, 0:P], rhs=zeros[:], start=True, stop=True)
 
         def transpose_in(x, part):
             bank = psum_tr.tile([P, 2, 256], F32, name="bank_in", tag="tr")
@@ -108,7 +108,7 @@ def tile_lstmcellunknowndata_pa_kernel(tc, hx, cx2, w1, b1, w2, b2, out):
 
         def copy_in(x, part, copy):
             if ("grouped", x) not in made:
-                made[("grouped", x)] = stage.tile([P, 2048], BF16, name="grouped", tag="grouped", align_bytes=64)
+                made[("grouped", x)] = staging.tile([P, 2048], BF16, name="grouped", tag="grouped", align_bytes=64)
             grouped_pairs = made[("grouped", x)][:].bitcast(F32)
             copy(out=grouped_pairs[:, part * 512:(part + 1) * 512].rearrange("q (r u) -> q r u", u=2),
                  in_=made[("bank_in", x, part)][:].rearrange("q u r -> q r u"))
@@ -172,7 +172,7 @@ def tile_lstmcellunknowndata_pa_kernel(tc, hx, cx2, w1, b1, w2, b2, out):
                 activate(layer, g, c, t, ALL)
 
         def regroup(g, c):
-            grouped = stage.tile([P, 512, 4], BF16, name="hidden_grouped", tag="hidden_grouped", align_bytes=64)
+            grouped = staging.tile([P, 512, 4], BF16, name="hidden_grouped", tag="hidden_grouped", align_bytes=64)
             made[("hidden_grouped", g, c)] = grouped
             nc.vector.tensor_copy(out=grouped[:].rearrange("p (r i) t -> p r t i", i=4),
                                   in_=made[("planes", g, c)][:].rearrange("p t (r i) -> p r t i", i=4))
@@ -264,22 +264,22 @@ def tile_lstmcellunknowndata_pa_kernel(tc, hx, cx2, w1, b1, w2, b2, out):
         nc.sync.dma_start(out=cx_sb[:], in_=cx2.rearrange("(p j) h -> p (j h)", j=8))
 
         for i in range(IDLE_MATMULS_BEFORE_FIRST_LOAD):
-            idle_matmul()
+            idle_matmul("head")
         transpose_in("w1_1", 0)
+        idle_matmul("head")
         copy_in("w1_1", 0, nc.scalar.copy)
         transpose_in("hx0", 0)
-        idle_matmul()
+        idle_matmul("head")
         copy_in("hx0", 0, nc.vector.tensor_copy)
         transpose_in("hx0", 1)
         copy_in("hx0", 1, nc.scalar.copy)
         bias_cast()
         bias_transpose()
-        idle_matmul()
         quantise_in("w1_1", 0)
         quantise_in("hx0", 0)
         bias_out()
         transpose_in("w1_1", 1)
-        idle_matmul()
+        idle_matmul("head")
         copy_in("w1_1", 1, nc.scalar.copy)
         quantise_in("hx0", 1)
         quantise_in("w1_1", 1)
@@ -342,19 +342,24 @@ def tile_lstmcellunknowndata_pa_kernel(tc, hx, cx2, w1, b1, w2, b2, out):
         layer_on(2, INPUT, 1)
         for jl in range(4):
             transpose_out(INPUT, 0, jl, psum_tr, "tr")
+            if jl % 2 == 1:
+                idle_matmul("end")
             add_and_store(jl, made[("bank_out", INPUT, 0, jl)][:], ALL)
 
         for jl in range(2):
             transpose_out(INPUT, 1, jl, psum_tr, "tr")
+            idle_matmul("end")
             sigmoid_stage(CANDIDATE, 1, FOUR, strip(jl))
         for jl in range(4):
-            pieces = (ALL,) if jl < 3 else (LEFT, RIGHT)
+            pieces = (ALL,) if jl < 2 else (LEFT, RIGHT)
             candidate_stage(1, FOUR, strip(jl))
             transpose_out(CANDIDATE, 1, jl, psum_mx, "mx")
+            idle_matmul("end")
             for cols in pieces:
                 late_sigmoid_stage(jl, cols)
             if jl < 2:
                 transpose_out(INPUT, 1, jl + 2, psum_tr, "tr")
+                idle_matmul("end")
                 sigmoid_stage(CANDIDATE, 1, FOUR, strip(jl + 2))
             for cols in pieces:
                 late_times_candidate(jl, cols)

@@ -93,10 +93,10 @@ def tile_lstmcellunknowndata_pa_kernel(tc, hx, cx2, w1, b1, w2, b2, out):
             x = "w2_%d" % g
             nc.sync.dma_start(out=raw[x].rearrange("p (t f) -> p t f", t=4), in_=dram[x])
 
-        def idle_matmul(phase):
-            if ("idle", phase) not in made:
-                made[("idle", phase)] = psum_mx.tile([P, 512], F32, name="idle", tag="mx")
-            nc.tensor.matmul(out=made[("idle", phase)][:], lhsT=zeros[:, 0:P], rhs=zeros[:], start=True, stop=True)
+        def idle_matmul():
+            if "idle" not in made:
+                made["idle"] = psum_mx.tile([P, 512], F32, name="idle", tag="mx")
+            nc.tensor.matmul(out=made["idle"][:], lhsT=zeros[:, 0:P], rhs=zeros[:], start=True, stop=True)
 
         def transpose_in(x, part):
             bank = psum_tr.tile([P, 2, 256], F32, name="bank_in", tag="tr")
@@ -264,12 +264,12 @@ def tile_lstmcellunknowndata_pa_kernel(tc, hx, cx2, w1, b1, w2, b2, out):
         nc.sync.dma_start(out=cx_sb[:], in_=cx2.rearrange("(p j) h -> p (j h)", j=8))
 
         for i in range(IDLE_MATMULS_BEFORE_FIRST_LOAD):
-            idle_matmul("head")
+            idle_matmul()
         transpose_in("w1_1", 0)
-        idle_matmul("head")
+        idle_matmul()
         copy_in("w1_1", 0, nc.scalar.copy)
         transpose_in("hx0", 0)
-        idle_matmul("head")
+        idle_matmul()
         copy_in("hx0", 0, nc.vector.tensor_copy)
         transpose_in("hx0", 1)
         copy_in("hx0", 1, nc.scalar.copy)
@@ -279,7 +279,7 @@ def tile_lstmcellunknowndata_pa_kernel(tc, hx, cx2, w1, b1, w2, b2, out):
         quantise_in("hx0", 0)
         bias_out()
         transpose_in("w1_1", 1)
-        idle_matmul("head")
+        idle_matmul()
         copy_in("w1_1", 1, nc.scalar.copy)
         quantise_in("hx0", 1)
         quantise_in("w1_1", 1)
@@ -342,24 +342,19 @@ def tile_lstmcellunknowndata_pa_kernel(tc, hx, cx2, w1, b1, w2, b2, out):
         layer_on(2, INPUT, 1)
         for jl in range(4):
             transpose_out(INPUT, 0, jl, psum_tr, "tr")
-            if jl % 2 == 1:
-                idle_matmul("end")
             add_and_store(jl, made[("bank_out", INPUT, 0, jl)][:], ALL)
 
         for jl in range(2):
             transpose_out(INPUT, 1, jl, psum_tr, "tr")
-            idle_matmul("end")
             sigmoid_stage(CANDIDATE, 1, FOUR, strip(jl))
         for jl in range(4):
             pieces = (ALL,) if jl < 2 else (LEFT, RIGHT)
             candidate_stage(1, FOUR, strip(jl))
             transpose_out(CANDIDATE, 1, jl, psum_mx, "mx")
-            idle_matmul("end")
             for cols in pieces:
                 late_sigmoid_stage(jl, cols)
             if jl < 2:
                 transpose_out(INPUT, 1, jl + 2, psum_tr, "tr")
-                idle_matmul("end")
                 sigmoid_stage(CANDIDATE, 1, FOUR, strip(jl + 2))
             for cols in pieces:
                 late_times_candidate(jl, cols)

from contextlib import ExitStack

import concourse.mybir as mybir
from concourse.masks import make_identity

FLOPS = 2 * 1024 * 512 * 512 * 6

F32 = mybir.dt.float32
BF16 = mybir.dt.bfloat16
U32 = mybir.dt.uint32
U8 = mybir.dt.uint8
FP8X4 = mybir.dt.float8_e4m3fn_x4
ACT = mybir.ActivationFunctionType
ALU = mybir.AluOpType

P = 128
INPUT = 0
FORGET = 1
CANDIDATE = 2
ALL = slice(0, 512)
LEFT = slice(0, 256)
RIGHT = slice(256, 512)
LOW = slice(0, 2)
HIGH = slice(2, 4)
FOUR = slice(0, 4)
IDLE_MATMULS_BEFORE_FIRST_LOAD = 5


def strip(jl):
    return slice(jl * P, (jl + 1) * P)


def tile_lstmcellunknowndata_pa_kernel(tc, hx, cx2, w1, b1, w2, b2, out):
    nc = tc.nc
    with ExitStack() as ctx:
        keep = ctx.enter_context(tc.tile_pool(name="keep", bufs=1))
        staging = ctx.enter_context(tc.tile_pool(name="stage", bufs=4))
        plane_pool = ctx.enter_context(tc.tile_pool(name="plane_pool", bufs=6))
        forget_pool = ctx.enter_context(tc.tile_pool(name="forget_pool", bufs=8))
        late_pool = ctx.enter_context(tc.tile_pool(name="late_pool", bufs=4))
        result_pool = ctx.enter_context(tc.tile_pool(name="result_pool", bufs=4))
        psum_mx = ctx.enter_context(tc.psum_pool(name="psum_mx", bufs=4))
        psum_tr = ctx.enter_context(tc.psum_pool(name="psum_tr", bufs=4))
        ctx.enter_context(tc.manual_schedule())

        hx_sb = keep.tile([P, 4096], BF16, name="hx_sb")
        cx_sb = keep.tile([P, 4096], BF16, name="cx_sb")
        hx_codes = keep.tile([P, 1024], U32, name="hx_codes", align_bytes=64)
        hx_scales = keep.tile([P, 1024], U8, name="hx_scales", align_bytes=64)
        hx_rows = hx.rearrange("(p j) k -> p (j k)", j=8)
        out_rows = out.rearrange("(p j) h -> p j h", j=8)
        raw = {}
        pairs = {}
        codes = {}
        scales = {}
        dram = {}
        for c in range(2):
            x = "hx%d" % c
            raw[x] = hx_sb[:, c * 2048:(c + 1) * 2048]
            pairs[x] = hx_sb[:].bitcast(F32)[:, c * 1024:(c + 1) * 1024]
            codes[x] = hx_codes[:, c * 512:(c + 1) * 512]
            scales[x] = hx_scales[:, c * 512:(c + 1) * 512]
            dram[x] = hx_rows[:, c * 2048:(c + 1) * 2048].rearrange("p (s r) -> p s r", s=2)
        for layer in (1, 2):
            for g in range(3):
                x = "w%d_%d" % (layer, g)
                w_sb = keep.tile([P, 2048], BF16, name="sb_" + x)
                w_codes = keep.tile([P, 512], U32, name="codes_" + x, align_bytes=64)
                w_scales = keep.tile([P, 512], U8, name="scales_" + x, align_bytes=64)
                raw[x] = w_sb[:]
                pairs[x] = w_sb[:].bitcast(F32)
                codes[x] = w_codes[:]
                scales[x] = w_scales[:]
        for g in range(3):
            dram["w1_%d" % g] = w1[g].rearrange("(u p e) k -> p u (e k)", u=2, e=2)
            dram["w2_%d" % g] = w2[g].rearrange("(t p) f -> p t f", p=P)

        b1_raw = keep.tile([P, 256], BF16, name="b1_raw")
        b2_raw = keep.tile([P, P], BF16, name="b2_raw")
        b2_f32 = keep.tile([P, P], F32, name="b2_f32")
        b1_pairs = keep.tile([P, 8], F32, name="b1_pairs")
        bias = {1: keep.tile([P, 12], F32, name="bias1"), 2: keep.tile([P, 12], F32, name="bias2")}
        zeros = keep.tile([P, 512], BF16, name="zeros")
        table_in = keep.tile([P, 1], F32, name="table_in")
        table_out = keep.tile([P, 1], F32, name="table_out")
        ident = keep.tile([P, P], F32, name="ident")
        made = {}

        def load_part(x, part):
            nc.sync.dma_start(out=raw[x][:, part * 1024:(part + 1) * 1024], in_=dram[x][:, part, :])

        def load_w2(g):
            x = "w2_%d" % g
            nc.sync.dma_start(out=raw[x].rearrange("p (t f) -> p t f", t=4), in_=dram[x])

        def idle_matmul():
            if "idle" not in made:
                made["idle"] = psum_mx.tile([P, 512], F32, name="idle", tag="mx")
            nc.tensor.matmul(out=made["idle"][:], lhsT=zeros[:, 0:P], rhs=zeros[:], start=True, stop=True)

        def transpose_in(x, part):
            bank = psum_tr.tile([P, 2, 256], F32, name="bank_in", tag="tr")
            made[("bank_in", x, part)] = bank
            for i in range(2):
                for u in range(2):
                    first = (2 * part + i) * 256 + u * P
                    nc.tensor.transpose(bank[:, u, i * P:(i + 1) * P], pairs[x][:, first:first + P], ident[:])

        def copy_in(x, part, copy):
            if ("grouped", x) not in made:
                made[("grouped", x)] = staging.tile([P, 2048], BF16, name="grouped", tag="grouped", align_bytes=64)
            grouped_pairs = made[("grouped", x)][:].bitcast(F32)
            copy(out=grouped_pairs[:, part * 512:(part + 1) * 512].rearrange("q (r u) -> q r u", u=2),
                 in_=made[("bank_in", x, part)][:].rearrange("q u r -> q r u"))

        def quantise_in(x, part):
            nc.vector.quantize_mx(out=codes[x][:, part * 256:(part + 1) * 256].bitcast(FP8X4),
                                  scales=scales[x][:, part * 256:(part + 1) * 256],
                                  in_=made[("grouped", x)][:, part * 1024:(part + 1) * 1024])

        def transpose_operand(x):
            for part in range(2):
                transpose_in(x, part)

        def prepare_on_vector(x):
            for part in range(2):
                copy_in(x, part, nc.vector.tensor_copy)
            for part in range(2):
                quantise_in(x, part)

        def bias_cast():
            nc.gpsimd.tensor_copy(out=b2_f32[:], in_=b2_raw[:])

        def bias_transpose():
            bank = psum_tr.tile([P, 2, P], F32, name="bank_bias", tag="tr")
            made["bank_bias"] = bank
            nc.tensor.transpose(bank[:, 0, :], b1_raw[:].bitcast(F32), ident[:])
            nc.tensor.transpose(bank[:, 1, :], b2_f32[:], ident[:])

        def bias_out():
            bank = made["bank_bias"]
            nc.vector.tensor_copy(out=b1_pairs[:, 0:6], in_=bank[:, 0, 0:6])
            nc.vector.tensor_copy(out=bias[2][:], in_=bank[:, 1, 0:12])
            nc.vector.tensor_copy(out=bias[1][:], in_=b1_pairs[:, 0:6].bitcast(BF16))

        def multiply(layer, g, c, t, cols):
            product = psum_mx.tile([P, 512 if cols == ALL else 256], F32, name="product", tag="mx")
            made[("product", layer, g, c, t, cols == RIGHT)] = product
            x = "w%d_%d" % (layer, g)
            if layer == 1:
                moving, moving_scales = codes["hx%d" % c], scales["hx%d" % c]
            else:
                moving, moving_scales = made[("hidden_codes", g, c)][:], made[("hidden_scales", g, c)][:]
            nc.tensor.matmul_mx(out=product[:], lhsT=codes[x][:, t * P:(t + 1) * P].bitcast(FP8X4),
                                lhsT_scale=scales[x][:, t * P:(t + 1) * P],
                                rhs=moving[:, cols].bitcast(FP8X4), rhs_scale=moving_scales[:, cols],
                                start=True, stop=True)

        def activate(layer, g, c, t, cols):
            key = ("planes", g, c) if layer == 1 else ("gate", g, c)
            if key not in made:
                if layer == 1:
                    made[key] = plane_pool.tile([P, 4, 512], BF16, name="planes", tag="planes")
                else:
                    made[key] = keep.tile([P, 4, 512], F32, name="gate%d%d" % (g, c))
            nc.scalar.activation(out=made[key][:, t, cols], in_=made[("product", layer, g, c, t, cols == RIGHT)][:],
                                 func=ACT.Tanh, bias=bias[layer][:, 4 * g + t:4 * g + t + 1], scale=1.0)

        def layer_on(layer, g, c):
            for t in range(4):
                multiply(layer, g, c, t, ALL)
                activate(layer, g, c, t, ALL)

        def regroup(g, c):
            grouped = staging.tile([P, 512, 4], BF16, name="hidden_grouped", tag="hidden_grouped", align_bytes=64)
            made[("hidden_grouped", g, c)] = grouped
            nc.vector.tensor_copy(out=grouped[:].rearrange("p (r i) t -> p r t i", i=4),
                                  in_=made[("planes", g, c)][:].rearrange("p t (r i) -> p r t i", i=4))

        def quantise_hidden(g, c):
            made[("hidden_codes", g, c)] = keep.tile([P, 512], U32, name="hidden_codes%d%d" % (g, c), align_bytes=64)
            made[("hidden_scales", g, c)] = keep.tile([P, 512], U8, name="hidden_scales%d%d" % (g, c), align_bytes=64)
            nc.vector.quantize_mx(out=made[("hidden_codes", g, c)][:].bitcast(FP8X4),
                                  scales=made[("hidden_scales", g, c)][:],
                                  in_=made[("hidden_grouped", g, c)][:].rearrange("p r t -> p (r t)"))

        def hidden_and_operand(g, c, x):
            regroup(g, c)
            copy_in(x, 0, nc.vector.tensor_copy)
            quantise_hidden(g, c)
            copy_in(x, 1, nc.vector.tensor_copy)
            quantise_in(x, 0)
            quantise_in(x, 1)

        def sigmoid_stage(g, c, tiles, cols):
            view = made[("gate", g, c)][:, tiles, cols]
            nc.scalar.activation(out=view, in_=view, func=ACT.Tanh, scale=0.5)

        def candidate_stage(c, tiles, cols):
            view = made[("gate", CANDIDATE, c)][:, tiles, cols]
            nc.scalar.activation(out=view, in_=view, func=ACT.Tanh, bias=0.5, scale=0.5)

        def in_two(stage_step, *unit):
            stage_step(*unit, LOW, ALL)
            stage_step(*unit, HIGH, ALL)

        def halve_cx():
            nc.vector.tensor_scalar_mul(out=cx_sb[:], in0=cx_sb[:], scalar1=0.5)

        def transpose_out(g, c, jl, pool, tag):
            bank = pool.tile([P, 512], F32, name="bank_out", tag=tag)
            made[("bank_out", g, c, jl)] = bank
            for t in range(4):
                nc.tensor.transpose(bank[:, t * P:(t + 1) * P], made[("gate", g, c)][:, t, strip(jl)], ident[:])

        def forget_term(c, jl):
            j = 4 * c + jl
            term = forget_pool.tile([P, 512], F32, name="forget_term", tag="forget_term")
            made[("forget_term", j)] = term
            nc.vector.scalar_tensor_tensor(out=term[:], in0=made[("bank_out", FORGET, c, jl)][:], scalar=1.0,
                                           in1=cx_sb[:, j * 512:(j + 1) * 512], op0=ALU.add, op1=ALU.mult)

        def input_times_candidate(c):
            view = made[("gate", INPUT, c)][:, :, :]
            nc.vector.scalar_tensor_tensor(out=view, in0=view, scalar=1.0, in1=made[("gate", CANDIDATE, c)][:, :, :],
                                           op0=ALU.add, op1=ALU.mult)

        def add_and_store(j, gated, cols):
            result = result_pool.tile([P, 512], F32, name="result", tag="result")
            nc.vector.scalar_tensor_tensor(out=result[:, cols], in0=gated, scalar=0.5,
                                           in1=made[("forget_term", j)][:, cols], op0=ALU.mult, op1=ALU.add)
            nc.sync.dma_start(out=out_rows[:, j, cols], in_=result[:, cols])

        def late_sigmoid_stage(jl, cols):
            if ("late", jl) not in made:
                made[("late", jl)] = late_pool.tile([P, 512], F32, name="late", tag="late")
            nc.scalar.activation(out=made[("late", jl)][:, cols], in_=made[("bank_out", INPUT, 1, jl)][:, cols],
                                 func=ACT.Tanh, scale=0.5)

        def late_times_candidate(jl, cols):
            view = made[("late", jl)][:, cols]
            nc.vector.scalar_tensor_tensor(out=view, in0=view, scalar=1.0,
                                           in1=made[("bank_out", CANDIDATE, 1, jl)][:, cols],
                                           op0=ALU.add, op1=ALU.mult)

        nc.vector.memset(zeros[:], 0.0)
        nc.vector.memset(b1_raw[:], 0.0)
        nc.vector.memset(b2_raw[:], 0.0)
        nc.vector.memset(table_in[:], 0.0)
        nc.scalar.activation(out=table_out[:], in_=table_in[:], func=ACT.Tanh)
        make_identity(nc, ident[:])

        load_part("w1_1", 0)
        load_part("hx0", 0)
        nc.sync.dma_start(out=b1_raw[0:6, :], in_=b1.rearrange("g (u r) -> (g u) r", u=2))
        nc.sync.dma_start(out=b2_raw[0:12, :], in_=b2.rearrange("g (t r) -> (g t) r", t=4))
        load_part("hx0", 1)
        load_part("w1_1", 1)
        for x in ("w1_2", "w1_0", "hx1"):
            load_part(x, 0)
            load_part(x, 1)
        for g in (FORGET, CANDIDATE, INPUT):
            load_w2(g)
        nc.sync.dma_start(out=cx_sb[:], in_=cx2.rearrange("(p j) h -> p (j h)", j=8))

        for i in range(IDLE_MATMULS_BEFORE_FIRST_LOAD):
            idle_matmul()
        transpose_in("w1_1", 0)
        idle_matmul()
        copy_in("w1_1", 0, nc.scalar.copy)
        transpose_in("hx0", 0)
        idle_matmul()
        copy_in("hx0", 0, nc.vector.tensor_copy)
        transpose_in("hx0", 1)
        copy_in("hx0", 1, nc.scalar.copy)
        bias_cast()
        bias_transpose()
        quantise_in("w1_1", 0)
        quantise_in("hx0", 0)
        bias_out()
        transpose_in("w1_1", 1)
        idle_matmul()
        copy_in("w1_1", 1, nc.scalar.copy)
        quantise_in("hx0", 1)
        quantise_in("w1_1", 1)
        transpose_in("w1_2", 0)

        for cols in (LEFT, RIGHT):
            for t in range(2):
                multiply(1, FORGET, 0, t, cols)
            if cols == LEFT:
                transpose_in("w1_2", 1)
            for t in range(2):
                activate(1, FORGET, 0, t, cols)
        for t in range(2, 4):
            multiply(1, FORGET, 0, t, ALL)
            activate(1, FORGET, 0, t, ALL)
        prepare_on_vector("w1_2")
        transpose_operand("w1_0")
        prepare_on_vector("w1_0")
        layer_on(1, CANDIDATE, 0)
        transpose_operand("hx1")
        prepare_on_vector("hx1")
        layer_on(1, INPUT, 0)
        transpose_operand("w2_1")
        hidden_and_operand(FORGET, 0, "w2_1")
        layer_on(1, FORGET, 1)
        regroup(FORGET, 1)
        halve_cx()
        quantise_hidden(FORGET, 1)
        layer_on(1, CANDIDATE, 1)
        layer_on(1, INPUT, 1)

        layer_on(2, FORGET, 0)
        in_two(sigmoid_stage, FORGET, 0)
        transpose_operand("w2_2")
        hidden_and_operand(CANDIDATE, 0, "w2_2")
        layer_on(2, FORGET, 1)
        in_two(sigmoid_stage, FORGET, 1)
        transpose_operand("w2_0")
        hidden_and_operand(INPUT, 0, "w2_0")
        for jl in range(4):
            transpose_out(FORGET, 0, jl, psum_tr, "tr")
        regroup(CANDIDATE, 1)
        forget_term(0, 0)
        quantise_hidden(CANDIDATE, 1)
        regroup(INPUT, 1)
        forget_term(0, 1)
        quantise_hidden(INPUT, 1)
        forget_term(0, 2)
        forget_term(0, 3)
        layer_on(2, CANDIDATE, 0)
        in_two(sigmoid_stage, CANDIDATE, 0)
        in_two(candidate_stage, 0)
        for jl in range(4):
            transpose_out(FORGET, 1, jl, psum_tr, "tr")
            forget_term(1, jl)
        layer_on(2, INPUT, 0)
        in_two(sigmoid_stage, INPUT, 0)
        input_times_candidate(0)
        layer_on(2, CANDIDATE, 1)
        layer_on(2, INPUT, 1)
        for jl in range(4):
            transpose_out(INPUT, 0, jl, psum_tr, "tr")
            add_and_store(jl, made[("bank_out", INPUT, 0, jl)][:], ALL)

        for jl in range(2):
            transpose_out(INPUT, 1, jl, psum_tr, "tr")
            sigmoid_stage(CANDIDATE, 1, FOUR, strip(jl))
        for jl in range(4):
            pieces = (ALL,) if jl < 2 else (LEFT, RIGHT)
            candidate_stage(1, FOUR, strip(jl))
            transpose_out(CANDIDATE, 1, jl, psum_mx, "mx")
            for cols in pieces:
                late_sigmoid_stage(jl, cols)
            if jl < 2:
                transpose_out(INPUT, 1, jl + 2, psum_tr, "tr")
                sigmoid_stage(CANDIDATE, 1, FOUR, strip(jl + 2))
            for cols in pieces:
                late_times_candidate(jl, cols)
            for cols in pieces:
                add_and_store(4 + jl, made[("late", jl)][:, cols], cols)
